import numpy as np
import ml_dtypes


def mxq(x, axis, fmt="e4m3"):
    dtype, down = {"e4m3": (ml_dtypes.float8_e4m3fn, 7), "e5m2": (ml_dtypes.float8_e5m2, 14)}[fmt]
    v = np.moveaxis(np.asarray(x, np.float32).astype(ml_dtypes.bfloat16).astype(np.float64), axis, -1)
    blocks = v.reshape(v.shape[:-1] + (-1, 32))
    amax = np.abs(blocks).max(-1, keepdims=True)
    byte = np.maximum(np.where(amax > 0, np.frexp(amax)[1] - 1 + 127, 0) - down, 1)
    scale = np.exp2(byte - 127.0)
    codes = (blocks / scale).astype(np.float32).astype(dtype).astype(np.float64)
    return np.moveaxis((codes * scale).reshape(v.shape), -1, axis)


WIDE = False


def mx_kscale(k):
    if not WIDE:
        return np.ones(k)
    levels = np.array([10, -10, 5, -5, 0])
    if k % 512:
        return np.exp2(np.random.permutation(np.resize(levels, k // 32))).repeat(32)
    a = np.empty((k // 512, 16))
    for p in range(k // 512):
        a[p, :8] = np.random.permutation(np.resize(levels, 8))
        for g in range(8):
            far = levels[np.abs(levels - a[p, g]) >= 10]
            a[p, g + 8] = far[np.random.randint(len(far))]
    return np.exp2(a.ravel()).repeat(32)


BF16 = ml_dtypes.bfloat16


def bf(x):
    return np.asarray(x, np.float32).astype(BF16)


def f64(x):
    return np.asarray(x).astype(np.float64)


B, T, D, H, QB = 1, 1024, 1024, 8, 512
DH = D // H
HP = H // 2
EPS = 1e-6
ROPE_BASE = 10000.0


def rmsnorm(u):
    return u / np.sqrt(np.mean(u * u, axis=-1, keepdims=True) + EPS)


def rope_tables():
    inv_freq = 1.0 / ROPE_BASE ** (np.arange(0, DH, 2) / DH)
    freqs = np.arange(T)[:, None] * inv_freq[None, :]
    return np.cos(freqs), np.sin(freqs)


def apply_rotary(u, cos, sin):
    d = DH // 2
    u1, u2 = u[..., :d], u[..., d:]
    c = cos[None, :, None, :]
    s = sin[None, :, None, :]
    return np.concatenate([u1 * c + u2 * s, -u1 * s + u2 * c], axis=-1)


def draw0():
    s = mx_kscale(D)
    return {"hidden_states": bf(np.random.standard_normal((B, T, D)) * s),
            "W_qkv": bf(np.random.standard_normal((D, 3 * D)) / np.sqrt(D) / s[:, None])}


def core(hidden_states, W_qkv):
    x = f64(hidden_states).reshape(B * T, D)
    qkv = mxq(x, 1, "e4m3") @ mxq(f64(W_qkv), 0, "e4m3")
    qkv = qkv.reshape(B, T, H, 3 * DH)
    q = qkv[..., :DH]
    k = qkv[..., DH:2 * DH]
    v = qkv[..., 2 * DH:]
    v = v.reshape(B, T, HP, 2 * DH)
    cos, sin = rope_tables()
    q = apply_rotary(rmsnorm(q), cos, sin)
    k = apply_rotary(rmsnorm(k), cos, sin)
    return q, k, v


def e4m3fn_bytes(y):
    return np.clip(np.asarray(y, np.float64), -448.0, 448.0).astype(np.float32).astype(ml_dtypes.float8_e4m3fn).view(np.uint8)


def e4m3fn_values(b):
    return np.asarray(b, np.uint8).view(ml_dtypes.float8_e4m3fn).astype(np.float64)


def setup_inputs():
    d = draw0()
    x0 = np.asarray(d['W_qkv']).astype(np.float64)
    s = (np.max(np.abs(x0), axis=(1,), keepdims=True) / 448.0).astype(np.float32)
    out = {}
    for k, v in d.items():
        if k == 'W_qkv':
            out['W_qkv_bytes'] = e4m3fn_bytes(x0 / s.astype(np.float64))
            out['W_qkv_scale'] = s
        else:
            out[k] = v
    return out


def reference(hidden_states, W_qkv_bytes, W_qkv_scale):
    return core(hidden_states, e4m3fn_values(W_qkv_bytes) * W_qkv_scale.astype(np.float64))

@@ -1,0 +1,295 @@
+import math
+from contextlib import ExitStack
+
+import concourse.mybir as mybir
+from concourse.masks import make_identity
+
+F32 = mybir.dt.float32
+BF16 = mybir.dt.bfloat16
+I32 = mybir.dt.int32
+U32 = mybir.dt.uint32
+U8 = mybir.dt.uint8
+FP8 = mybir.dt.float8_e4m3fn
+FP8X4 = mybir.dt.float8_e4m3fn_x4
+ALU = mybir.AluOpType
+ACT = mybir.ActivationFunctionType
+
+P = 128
+T = 1024
+D = 1024
+H = 8
+DH = 128
+HALF = 64
+NT = T // P
+NG = D // 512
+NCOL = 3 * D
+QW = NCOL // 4
+BANK = 512
+EPS = 1e-6
+
+FLOPS = 2 * T * D * NCOL
+
+TWO_PI = 2.0 * math.pi
+C1 = 6.28125
+C2 = TWO_PI - C1
+MAGIC = 12582912.0
+
+NQ = 4
+POOL_ADDS = True
+X_COPY_ON_VECTOR = True
+WIDEN_ON_VECTOR = ()
+WIDEN_PER_STEP = (3, 3, 3, 3, 3, 3, 3, 3, 0, 0, 0, 0, 0, 0, 0, 0)
+
+
+def tile_mixerdiffattention_pa_kernel(tc, hidden_states, W_qkv_bytes, W_qkv_scale, out_0, out_1, out_2):
+    nc = tc.nc
+    x_dram = hidden_states.rearrange("b t k -> (b t) k")
+    w_dram = W_qkv_bytes.rearrange("(g p t) n -> g p t n", g=NG, p=P, t=4)
+    s_dram = W_qkv_scale.rearrange("(g p t) o -> p g (t o)", g=NG, p=P, t=4)
+    outs = [
+        out_0.rearrange("b t h d -> (b t) (h d)"),
+        out_1.rearrange("b t h d -> (b t) (h d)"),
+        out_2.rearrange("b t h d -> (b t) (h d)"),
+    ]
+
+    with ExitStack() as ctx:
+        keep = ctx.enter_context(tc.tile_pool(name="keep", bufs=1))
+        work = ctx.enter_context(tc.tile_pool(name="work", bufs=2))
+        stage = ctx.enter_context(tc.tile_pool(name="stage", bufs=4))
+        store = ctx.enter_context(tc.tile_pool(name="store", bufs=4))
+        psum = ctx.enter_context(tc.psum_pool(name="psum", bufs=8))
+
+        wsc = keep.tile([P, NG, 4], F32, name="wsc")
+        nc.sync.dma_start(out=wsc[:], in_=s_dram)
+        wbytes = [keep.tile([P, 4, NCOL], U8, name="wbytes%d" % g) for g in range(NG)]
+        x_all = keep.tile([P, NT, D], BF16, name="x_all")
+
+        def load_w(g, c0, c1):
+            nc.sync.dma_start(out=wbytes[g][:, :, c0:c1], in_=w_dram[g][:, :, c0:c1])
+
+        def load_x(a0, n):
+            nc.sync.dma_start(
+                out=x_all[:, a0 : a0 + n, :],
+                in_=x_dram[a0 * P : (a0 + n) * P, :].rearrange("(a p) k -> p a k", p=P),
+            )
+
+        load_w(0, 0, QW)
+        load_w(1, 0, QW)
+        load_x(0, 2)
+        load_x(2, 2)
+        load_w(0, QW, 2 * QW)
+        load_w(1, QW, 2 * QW)
+        load_x(4, 2)
+        load_x(6, 2)
+        load_w(0, 2 * QW, 4 * QW)
+        load_w(1, 2 * QW, 4 * QW)
+
+        warm = keep.tile([P, 1], F32, name="warm")
+        nc.vector.memset(warm[:], 0.0)
+        nc.scalar.activation(out=warm[:], in_=warm[:], func=ACT.Sin)
+        freq = keep.tile([P, HALF], F32, name="freq")
+        nc.vector.memset(freq[:, 0:1], 1.0)
+        for b in range(6):
+            n = 2**b
+            nc.vector.tensor_scalar(
+                out=freq[:, n : 2 * n], in0=freq[:, 0:n], scalar1=10000.0 ** (-n / 64.0), scalar2=None, op0=ALU.mult
+            )
+        tpos = keep.tile([P, NT], F32, name="tpos")
+        nc.gpsimd.iota(tpos[:], pattern=[[P, NT]], base=0, channel_multiplier=1, allow_small_or_imprecise_dtypes=True)
+        ident = keep.tile([P, P], F32, name="ident")
+        make_identity(nc, ident[:])
+        NA = NT * HALF
+        theta = keep.tile([P, NT, HALF], F32, name="theta")
+        nc.vector.tensor_tensor(
+            out=theta[:],
+            in0=freq[:].unsqueeze(1).to_broadcast([P, NT, HALF]),
+            in1=tpos[:].unsqueeze(2).to_broadcast([P, NT, HALF]),
+            op=ALU.mult,
+        )
+        theta_f = theta[:].rearrange("p a j -> p (a j)")
+        turns = keep.tile([P, 2, NA], F32, name="turns")
+        nc.vector.tensor_scalar(out=turns[:, 0, :], in0=theta_f, scalar1=1.0 / TWO_PI, scalar2=None, op0=ALU.mult)
+        nc.vector.tensor_scalar(
+            out=turns[:, 1, :], in0=theta_f, scalar1=1.0 / TWO_PI, scalar2=-0.25, op0=ALU.mult, op1=ALU.add
+        )
+        whole = keep.tile([P, 2, NA], I32, name="whole")
+        nc.vector.tensor_scalar(out=whole[:], in0=turns[:], scalar1=MAGIC, scalar2=MAGIC, op0=ALU.add, op1=ALU.subtract)
+        rest = keep.tile([P, 2, NA], F32, name="rest")
+        nc.vector.scalar_tensor_tensor(
+            out=rest[:],
+            in0=whole[:],
+            scalar=-C1,
+            in1=theta_f.unsqueeze(1).to_broadcast([P, 2, NA]),
+            op0=ALU.mult,
+            op1=ALU.add,
+        )
+        nc.vector.scalar_tensor_tensor(out=rest[:], in0=whole[:], scalar=-C2, in1=rest[:], op0=ALU.mult, op1=ALU.add)
+        mag = keep.tile([P, 2, NT, HALF], F32, name="mag")
+        cs = keep.tile([P, NT, 4, HALF], F32, name="cs")
+
+        def tables_on_scalar():
+            nc.scalar.activation(out=mag[:, 0].rearrange("p a j -> p (a j)"), in_=rest[:, 0, :], func=ACT.Abs)
+            nc.scalar.activation(
+                out=mag[:, 1].rearrange("p a j -> p (a j)"), in_=rest[:, 1, :], func=ACT.Abs, bias=-0.5 * math.pi
+            )
+            nc.scalar.activation(out=cs[:, :, 0, :], in_=mag[:, 0], func=ACT.Sin, scale=-1.0, bias=0.5 * math.pi)
+            nc.scalar.activation(out=cs[:, :, 3, :], in_=mag[:, 0], func=ACT.Sin, scale=-1.0, bias=0.5 * math.pi)
+            nc.scalar.activation(out=cs[:, :, 1, :], in_=mag[:, 1], func=ACT.Sin, scale=-1.0, bias=0.5 * math.pi)
+            nc.scalar.activation(out=cs[:, :, 2, :], in_=mag[:, 1], func=ACT.Sin, scale=1.0, bias=-0.5 * math.pi)
+
+        xc = keep.tile([P, NT, NG * P], U32, name="xc", align_bytes=64)
+        xs = keep.tile([P, NT, NG * P], U8, name="xs", align_bytes=64)
+
+        def x_prep(a):
+            words = x_all[:, a, :].bitcast(F32)
+            xt = psum.tile([P, NG, 2, P], F32, name="xt", tag="bank")
+            for g in range(NG):
+                for u in range(2):
+                    nc.tensor.transpose(xt[:, g, u, :], words[:, 256 * g + u : 256 * (g + 1) : 2], ident[:])
+            xg = work.tile([P, NG * P * 4], BF16, name="xg", align_bytes=64)
+            dst = xg[:].bitcast(F32).rearrange("p (g r u) -> p g r u", g=NG, u=2)
+            src = xt[:].rearrange("p g u r -> p g r u")
+            if X_COPY_ON_VECTOR:
+                nc.vector.tensor_copy(out=dst, in_=src)
+            else:
+                nc.scalar.copy(out=dst, in_=src)
+            nc.vector.quantize_mx(out=xc[:, a, :].bitcast(FP8X4), scales=xs[:, a, :], in_=xg[:])
+
+        wide = [keep.tile([P, NG, 4, QW], BF16, name="wide%d" % qq) for qq in range(NQ)]
+        wcodes = keep.tile([P, NQ, NG * QW], U32, name="wcodes", align_bytes=64)
+        wscl = keep.tile([P, NQ, NG * QW], U8, name="wscl", align_bytes=64)
+        grouped = {}
+
+        def widen(qq, g, t):
+            src = wbytes[g][:, t, qq * QW : (qq + 1) * QW].bitcast(FP8)
+            if (qq, g, t) in WIDEN_ON_VECTOR:
+                nc.vector.tensor_scalar(
+                    out=wide[qq][:, g, t, :], in0=src, scalar1=wsc[:, g, t : t + 1], scalar2=None, op0=ALU.mult
+                )
+            else:
+                nc.scalar.activation(out=wide[qq][:, g, t, :], in_=src, func=ACT.Copy, scale=wsc[:, g, t : t + 1])
+
+        def interleave(qq, g):
+            if g == 0:
+                gr = work.tile([P, NG, QW * 4], BF16, name="grouped", align_bytes=64)
+                grouped[qq] = gr
+            for ty in range(3):
+                nc.vector.tensor_copy(
+                    out=grouped[qq][:, g, ty * 1024 : (ty + 1) * 1024].rearrange("p (i d t) -> p i d t", i=2, d=DH, t=4),
+                    in_=wide[qq][:, g].rearrange("p t (i y d) -> p y i d t", i=2, y=3, d=DH)[:, ty],
+                )
+
+        def w_quant(qq):
+            flat = grouped[qq][:].rearrange("p g c -> p (g c)")
+            for c0, c1 in ((0, 1024), (1024, 1536)):
+                nc.vector.quantize_mx(
+                    out=wcodes[:, qq, c0:c1].bitcast(FP8X4), scales=wscl[:, qq, c0:c1], in_=flat[:, 4 * c0 : 4 * c1]
+                )
+
+        junk = keep.tile([P, DH], BF16, name="junk")
+
+        def mx(out, a, qq, c0, c1):
+            for g in range(NG):
+                nc.tensor.matmul_mx(
+                    out=out,
+                    lhsT=xc[:, a, g * P : (g + 1) * P].bitcast(FP8X4),
+                    lhsT_scale=xs[:, a, g * P : (g + 1) * P],
+                    rhs=wcodes[:, qq, g * QW + c0 : g * QW + c1].bitcast(FP8X4),
+                    rhs_scale=wscl[:, qq, g * QW + c0 : g * QW + c1],
+                    start=(g == 0),
+                    stop=(g == NG - 1),
+                )
+
+        def step(j, qq, fill_scalar, fill_vector):
+            a0 = 2 * j
+            accs = []
+            for e in range(2):
+                acc = psum.tile([P, BANK], F32, name="acc", tag="bank")
+                mx(acc[:], a0 + e, qq, 0, BANK)
+                accs.append(acc)
+            accv = psum.tile([P, 2, 256], F32, name="accv", tag="bank")
+            for e in range(2):
+                mx(accv[:, e, :], a0 + e, qq, BANK, QW)
+            rns = []
+            for e in range(2):
+                ss = stage.tile([P, 4], F32, name="ss")
+                for i in range(4):
+                    nc.scalar.activation(
+                        out=junk[:], in_=accs[e][:, i * DH : (i + 1) * DH], func=ACT.Square, accum_out=ss[:, i : i + 1]
+                    )
+                rt = stage.tile([P, 4], F32, name="rt")
+                nc.scalar.activation(out=rt[:], in_=ss[:], func=ACT.Sqrt, scale=1.0 / DH, bias=EPS)
+                rn = stage.tile([P, 4], F32, name="rn")
+                nc.vector.reciprocal(out=rn[:], in_=rt[:])
+                rns.append(rn)
+            rows = slice(a0 * P, (a0 + 2) * P)
+            cols = slice(qq * 256, (qq + 1) * 256)
+            ov = store.tile([P, 2, 256], F32, name="ov")
+            nc.scalar.copy(out=ov[:], in_=accv[:])
+            nc.sync.dma_start(out=outs[2][rows, cols].rearrange("(e p) c -> p e c", p=P), in_=ov[:])
+            fill_scalar()
+            o = store.tile([P, 2, BANK], F32, name="o")
+            for e in range(2):
+                pq = stage.tile([P, 4, 4 * HALF], F32, name="pq")
+                for i in range(4):
+                    nc.vector.scalar_tensor_tensor(
+                        out=pq[:, i, :].rearrange("p (r c) -> p r c", r=2),
+                        in0=accs[e][:, i * DH : (i + 1) * DH].unsqueeze(1).to_broadcast([P, 2, DH]),
+                        scalar=rns[e][:, i : i + 1],
+                        in1=cs[:, a0 + e].rearrange("p (r b) j -> p r (b j)", r=2),
+                        op0=ALU.mult,
+                        op1=ALU.mult,
+                    )
+                pairs = pq[:].rearrange("p i (h b j) -> p (i h) b j", h=2, b=2)
+                eng = nc.gpsimd if POOL_ADDS else nc.vector
+                eng.tensor_tensor(
+                    out=o[:, e, :].rearrange("p (m j) -> p m j", j=HALF),
+                    in0=pairs[:, :, 0, :],
+                    in1=pairs[:, :, 1, :],
+                    op=ALU.add,
+                )
+            for ty in range(2):
+                nc.sync.dma_start(
+                    out=outs[ty][rows, cols].rearrange("(e p) c -> p e c", p=P), in_=o[:, :, ty * 256 : (ty + 1) * 256]
+                )
+            fill_vector()
+
+        for t in range(4):
+            widen(0, 0, t)
+        x_prep(0)
+        x_prep(1)
+        interleave(0, 0)
+        for t in range(4):
+            widen(0, 1, t)
+        tables_on_scalar()
+        interleave(0, 1)
+        w_quant(0)
+
+        todo = [(qq, g, t) for qq in range(1, NQ) for g in range(NG) for t in range(4)]
+        done = [0]
+        made = [0, 0]
+
+        def fill_scalar_for(s):
+            def fill():
+                for k in range(WIDEN_PER_STEP[s]):
+                    widen(*todo[done[0]])
+                    done[0] += 1
+
+            return fill
+
+        def fill_vector():
+            if made[1] < NQ - 1 and made[0] >= 2 * (made[1] + 1):
+                w_quant(1 + made[1])
+                made[1] += 1
+            elif made[0] < 2 * (NQ - 1) and done[0] >= 4 * (made[0] + 1):
+                interleave(1 + made[0] // 2, made[0] % 2)
+                made[0] += 1
+
+        for qq in range(NQ):
+            for j in range(4):
+                while made[1] < qq:
+                    fill_vector()
+                if qq == 0 and j < 3:
+                    x_prep(2 * j + 2)
+                    x_prep(2 * j + 3)
+                step(j, qq, fill_scalar_for(4 * qq + j), fill_vector)

@@ -35,7 +35,7 @@ C2 = TWO_PI - C1
 MAGIC = 12582912.0
 
 NQ = 4
-POOL_ADDS = True
+POOL_ADDS = False
 X_COPY_ON_VECTOR = True
 WIDEN_ON_VECTOR = ()
 WIDEN_PER_STEP = (3, 3, 3, 3, 3, 3, 3, 3, 0, 0, 0, 0, 0, 0, 0, 0)

@@ -35,10 +35,11 @@ C2 = TWO_PI - C1
 MAGIC = 12582912.0
 
 NQ = 4
-POOL_ADDS = False
+POOL_ADDS = True
 X_COPY_ON_VECTOR = True
-WIDEN_ON_VECTOR = ()
-WIDEN_PER_STEP = (3, 3, 3, 3, 3, 3, 3, 3, 0, 0, 0, 0, 0, 0, 0, 0)
+WIDEN_ON_VECTOR = tuple((qq, 1, t) for qq in range(4) for t in range(4))
+WIDEN_PER_STEP = (4, 4, 2, 2, 2, 2, 2, 2, 2, 2, 0, 0, 0, 0, 0, 0)
+QUANT_AFTER = (1, 2)
 
 
 def tile_mixerdiffattention_pa_kernel(tc, hidden_states, W_qkv_bytes, W_qkv_scale, out_0, out_1, out_2):
@@ -107,30 +108,22 @@ def tile_mixerdiffattention_pa_kernel(tc, hidden_states, W_qkv_bytes, W_qkv_scal
             op=ALU.mult,
         )
         theta_f = theta[:].rearrange("p a j -> p (a j)")
-        turns = keep.tile([P, 2, NA], F32, name="turns")
-        nc.vector.tensor_scalar(out=turns[:, 0, :], in0=theta_f, scalar1=1.0 / TWO_PI, scalar2=None, op0=ALU.mult)
+        turns = keep.tile([P, NA], F32, name="turns")
         nc.vector.tensor_scalar(
-            out=turns[:, 1, :], in0=theta_f, scalar1=1.0 / TWO_PI, scalar2=-0.25, op0=ALU.mult, op1=ALU.add
+            out=turns[:], in0=theta_f, scalar1=1.0 / TWO_PI, scalar2=-0.125, op0=ALU.mult, op1=ALU.add
         )
-        whole = keep.tile([P, 2, NA], I32, name="whole")
+        whole = keep.tile([P, NA], I32, name="whole")
         nc.vector.tensor_scalar(out=whole[:], in0=turns[:], scalar1=MAGIC, scalar2=MAGIC, op0=ALU.add, op1=ALU.subtract)
-        rest = keep.tile([P, 2, NA], F32, name="rest")
-        nc.vector.scalar_tensor_tensor(
-            out=rest[:],
-            in0=whole[:],
-            scalar=-C1,
-            in1=theta_f.unsqueeze(1).to_broadcast([P, 2, NA]),
-            op0=ALU.mult,
-            op1=ALU.add,
-        )
+        rest = keep.tile([P, NA], F32, name="rest")
+        nc.vector.scalar_tensor_tensor(out=rest[:], in0=whole[:], scalar=-C1, in1=theta_f, op0=ALU.mult, op1=ALU.add)
         nc.vector.scalar_tensor_tensor(out=rest[:], in0=whole[:], scalar=-C2, in1=rest[:], op0=ALU.mult, op1=ALU.add)
         mag = keep.tile([P, 2, NT, HALF], F32, name="mag")
         cs = keep.tile([P, NT, 4, HALF], F32, name="cs")
 
         def tables_on_scalar():
-            nc.scalar.activation(out=mag[:, 0].rearrange("p a j -> p (a j)"), in_=rest[:, 0, :], func=ACT.Abs)
+            nc.scalar.activation(out=mag[:, 0].rearrange("p a j -> p (a j)"), in_=rest[:], func=ACT.Abs)
             nc.scalar.activation(
-                out=mag[:, 1].rearrange("p a j -> p (a j)"), in_=rest[:, 1, :], func=ACT.Abs, bias=-0.5 * math.pi
+                out=mag[:, 1].rearrange("p a j -> p (a j)"), in_=rest[:], func=ACT.Abs, bias=-0.5 * math.pi
             )
             nc.scalar.activation(out=cs[:, :, 0, :], in_=mag[:, 0], func=ACT.Sin, scale=-1.0, bias=0.5 * math.pi)
             nc.scalar.activation(out=cs[:, :, 3, :], in_=mag[:, 0], func=ACT.Sin, scale=-1.0, bias=0.5 * math.pi)
@@ -158,7 +151,6 @@ def tile_mixerdiffattention_pa_kernel(tc, hidden_states, W_qkv_bytes, W_qkv_scal
         wide = [keep.tile([P, NG, 4, QW], BF16, name="wide%d" % qq) for qq in range(NQ)]
         wcodes = keep.tile([P, NQ, NG * QW], U32, name="wcodes", align_bytes=64)
         wscl = keep.tile([P, NQ, NG * QW], U8, name="wscl", align_bytes=64)
-        grouped = {}
 
         def widen(qq, g, t):
             src = wbytes[g][:, t, qq * QW : (qq + 1) * QW].bitcast(FP8)
@@ -169,21 +161,18 @@ def tile_mixerdiffattention_pa_kernel(tc, hidden_states, W_qkv_bytes, W_qkv_scal
             else:
                 nc.scalar.activation(out=wide[qq][:, g, t, :], in_=src, func=ACT.Copy, scale=wsc[:, g, t : t + 1])
 
-        def interleave(qq, g):
-            if g == 0:
-                gr = work.tile([P, NG, QW * 4], BF16, name="grouped", align_bytes=64)
-                grouped[qq] = gr
+        def w_quant(qq, g):
+            grouped = work.tile([P, QW * 4], BF16, name="grouped", align_bytes=64)
             for ty in range(3):
                 nc.vector.tensor_copy(
-                    out=grouped[qq][:, g, ty * 1024 : (ty + 1) * 1024].rearrange("p (i d t) -> p i d t", i=2, d=DH, t=4),
+                    out=grouped[:, ty * 1024 : (ty + 1) * 1024].rearrange("p (i d t) -> p i d t", i=2, d=DH, t=4),
                     in_=wide[qq][:, g].rearrange("p t (i y d) -> p y i d t", i=2, y=3, d=DH)[:, ty],
                 )
-
-        def w_quant(qq):
-            flat = grouped[qq][:].rearrange("p g c -> p (g c)")
-            for c0, c1 in ((0, 1024), (1024, 1536)):
+            for c0, c1 in ((0, 512), (512, 768)):
                 nc.vector.quantize_mx(
-                    out=wcodes[:, qq, c0:c1].bitcast(FP8X4), scales=wscl[:, qq, c0:c1], in_=flat[:, 4 * c0 : 4 * c1]
+                    out=wcodes[:, qq, g * QW + c0 : g * QW + c1].bitcast(FP8X4),
+                    scales=wscl[:, qq, g * QW + c0 : g * QW + c1],
+                    in_=grouped[:, 4 * c0 : 4 * c1],
                 )
 
         junk = keep.tile([P, DH], BF16, name="junk")
@@ -200,7 +189,7 @@ def tile_mixerdiffattention_pa_kernel(tc, hidden_states, W_qkv_bytes, W_qkv_scal
                     stop=(g == NG - 1),
                 )
 
-        def step(j, qq, fill_scalar, fill_vector):
+        def step(j, qq, fill_scalar, fill_middle, fill_vector):
             a0 = 2 * j
             accs = []
             for e in range(2):
@@ -228,6 +217,7 @@ def tile_mixerdiffattention_pa_kernel(tc, hidden_states, W_qkv_bytes, W_qkv_scal
             nc.scalar.copy(out=ov[:], in_=accv[:])
             nc.sync.dma_start(out=outs[2][rows, cols].rearrange("(e p) c -> p e c", p=P), in_=ov[:])
             fill_scalar()
+            fill_middle()
             o = store.tile([P, 2, BANK], F32, name="o")
             for e in range(2):
                 pq = stage.tile([P, 4, 4 * HALF], F32, name="pq")
@@ -258,16 +248,14 @@ def tile_mixerdiffattention_pa_kernel(tc, hidden_states, W_qkv_bytes, W_qkv_scal
             widen(0, 0, t)
         x_prep(0)
         x_prep(1)
-        interleave(0, 0)
+        w_quant(0, 0)
         for t in range(4):
             widen(0, 1, t)
         tables_on_scalar()
-        interleave(0, 1)
-        w_quant(0)
+        w_quant(0, 1)
 
         todo = [(qq, g, t) for qq in range(1, NQ) for g in range(NG) for t in range(4)]
         done = [0]
-        made = [0, 0]
 
         def fill_scalar_for(s):
             def fill():
@@ -277,19 +265,20 @@ def tile_mixerdiffattention_pa_kernel(tc, hidden_states, W_qkv_bytes, W_qkv_scal
 
             return fill
 
-        def fill_vector():
-            if made[1] < NQ - 1 and made[0] >= 2 * (made[1] + 1):
-                w_quant(1 + made[1])
-                made[1] += 1
-            elif made[0] < 2 * (NQ - 1) and done[0] >= 4 * (made[0] + 1):
-                interleave(1 + made[0] // 2, made[0] % 2)
-                made[0] += 1
+        def fill_middle_for(s):
+            def fill():
+                if s < 3:
+                    x_prep(2 * s + 2)
+                    x_prep(2 * s + 3)
 
-        for qq in range(NQ):
-            for j in range(4):
-                while made[1] < qq:
-                    fill_vector()
-                if qq == 0 and j < 3:
-                    x_prep(2 * j + 2)
-                    x_prep(2 * j + 3)
-                step(j, qq, fill_scalar_for(4 * qq + j), fill_vector)
+            return fill
+
+        def fill_vector_for(s):
+            def fill():
+                if s // 4 < NQ - 1 and s % 4 in QUANT_AFTER:
+                    w_quant(s // 4 + 1, QUANT_AFTER.index(s % 4))
+
+            return fill
+
+        for s in range(4 * NQ):
+            step(s % 4, s // 4, fill_scalar_for(s), fill_middle_for(s), fill_vector_for(s))

@@ -231,7 +231,7 @@ def tile_mixerdiffattention_pa_kernel(tc, hidden_states, W_qkv_bytes, W_qkv_scal
                         op1=ALU.mult,
                     )
                 pairs = pq[:].rearrange("p i (h b j) -> p (i h) b j", h=2, b=2)
-                eng = nc.gpsimd if POOL_ADDS else nc.vector
+                eng = nc.gpsimd if (POOL_ADDS and e == 0) else nc.vector
                 eng.tensor_tensor(
                     out=o[:, e, :].rearrange("p (m j) -> p m j", j=HALF),
                     in0=pairs[:, :, 0, :],

@@ -17,13 +17,12 @@ ACT = mybir.ActivationFunctionType
 P = 128
 T = 1024
 D = 1024
-H = 8
 DH = 128
 HALF = 64
 NT = T // P
 NG = D // 512
 NCOL = 3 * D
-QW = NCOL // 4
+HW = NCOL // 2
 BANK = 512
 EPS = 1e-6
 
@@ -34,12 +33,8 @@ C1 = 6.28125
 C2 = TWO_PI - C1
 MAGIC = 12582912.0
 
-NQ = 4
-POOL_ADDS = True
-X_COPY_ON_VECTOR = True
-WIDEN_ON_VECTOR = tuple((qq, 1, t) for qq in range(4) for t in range(4))
-WIDEN_PER_STEP = (4, 4, 2, 2, 2, 2, 2, 2, 2, 2, 0, 0, 0, 0, 0, 0)
-QUANT_AFTER = (1, 2)
+UNITS = ((0, 0), (0, 1), (1, 0), (1, 1))
+WIDEN_ON_VECTOR = ((0, 1), (0, 2), (0, 3), (3, 3))
 
 
 def tile_mixerdiffattention_pa_kernel(tc, hidden_states, W_qkv_bytes, W_qkv_scale, out_0, out_1, out_2):
@@ -55,18 +50,23 @@ def tile_mixerdiffattention_pa_kernel(tc, hidden_states, W_qkv_bytes, W_qkv_scal
 
     with ExitStack() as ctx:
         keep = ctx.enter_context(tc.tile_pool(name="keep", bufs=1))
-        work = ctx.enter_context(tc.tile_pool(name="work", bufs=2))
+        work = ctx.enter_context(tc.tile_pool(name="work", bufs=3))
+        xwork = ctx.enter_context(tc.tile_pool(name="xwork", bufs=4))
         stage = ctx.enter_context(tc.tile_pool(name="stage", bufs=4))
-        store = ctx.enter_context(tc.tile_pool(name="store", bufs=4))
+        store = ctx.enter_context(tc.tile_pool(name="store", bufs=6))
         psum = ctx.enter_context(tc.psum_pool(name="psum", bufs=8))
+        ctx.enter_context(tc.manual_schedule())
 
         wsc = keep.tile([P, NG, 4], F32, name="wsc")
         nc.sync.dma_start(out=wsc[:], in_=s_dram)
         wbytes = [keep.tile([P, 4, NCOL], U8, name="wbytes%d" % g) for g in range(NG)]
         x_all = keep.tile([P, NT, D], BF16, name="x_all")
 
-        def load_w(g, c0, c1):
-            nc.sync.dma_start(out=wbytes[g][:, :, c0:c1], in_=w_dram[g][:, :, c0:c1])
+        def load_w(u):
+            half, g = UNITS[u]
+            nc.sync.dma_start(
+                out=wbytes[g][:, :, half * HW : (half + 1) * HW], in_=w_dram[g][:, :, half * HW : (half + 1) * HW]
+            )
 
         def load_x(a0, n):
             nc.sync.dma_start(
@@ -74,16 +74,14 @@ def tile_mixerdiffattention_pa_kernel(tc, hidden_states, W_qkv_bytes, W_qkv_scal
                 in_=x_dram[a0 * P : (a0 + n) * P, :].rearrange("(a p) k -> p a k", p=P),
             )
 
-        load_w(0, 0, QW)
-        load_w(1, 0, QW)
+        load_w(0)
+        load_w(1)
         load_x(0, 2)
         load_x(2, 2)
-        load_w(0, QW, 2 * QW)
-        load_w(1, QW, 2 * QW)
+        load_w(2)
         load_x(4, 2)
         load_x(6, 2)
-        load_w(0, 2 * QW, 4 * QW)
-        load_w(1, 2 * QW, 4 * QW)
+        load_w(3)
 
         warm = keep.tile([P, 1], F32, name="warm")
         nc.vector.memset(warm[:], 0.0)
@@ -117,14 +115,23 @@ def tile_mixerdiffattention_pa_kernel(tc, hidden_states, W_qkv_bytes, W_qkv_scal
         rest = keep.tile([P, NA], F32, name="rest")
         nc.vector.scalar_tensor_tensor(out=rest[:], in0=whole[:], scalar=-C1, in1=theta_f, op0=ALU.mult, op1=ALU.add)
         nc.vector.scalar_tensor_tensor(out=rest[:], in0=whole[:], scalar=-C2, in1=rest[:], op0=ALU.mult, op1=ALU.add)
+        shifted = keep.tile([P, NA], F32, name="shifted")
+        nc.vector.tensor_scalar(out=shifted[:], in0=rest[:], scalar1=-0.5 * math.pi, scalar2=None, op0=ALU.add)
         mag = keep.tile([P, 2, NT, HALF], F32, name="mag")
+        nc.vector.scalar_tensor_tensor(
+            out=mag[:, 0].rearrange("p a j -> p (a j)"), in0=rest[:], scalar=-1.0, in1=rest[:], op0=ALU.mult, op1=ALU.max
+        )
+        nc.vector.scalar_tensor_tensor(
+            out=mag[:, 1].rearrange("p a j -> p (a j)"),
+            in0=shifted[:],
+            scalar=-1.0,
+            in1=shifted[:],
+            op0=ALU.mult,
+            op1=ALU.max,
+        )
         cs = keep.tile([P, NT, 4, HALF], F32, name="cs")
 
         def tables_on_scalar():
-            nc.scalar.activation(out=mag[:, 0].rearrange("p a j -> p (a j)"), in_=rest[:], func=ACT.Abs)
-            nc.scalar.activation(
-                out=mag[:, 1].rearrange("p a j -> p (a j)"), in_=rest[:], func=ACT.Abs, bias=-0.5 * math.pi
-            )
             nc.scalar.activation(out=cs[:, :, 0, :], in_=mag[:, 0], func=ACT.Sin, scale=-1.0, bias=0.5 * math.pi)
             nc.scalar.activation(out=cs[:, :, 3, :], in_=mag[:, 0], func=ACT.Sin, scale=-1.0, bias=0.5 * math.pi)
             nc.scalar.activation(out=cs[:, :, 1, :], in_=mag[:, 1], func=ACT.Sin, scale=-1.0, bias=0.5 * math.pi)
@@ -132,153 +139,153 @@ def tile_mixerdiffattention_pa_kernel(tc, hidden_states, W_qkv_bytes, W_qkv_scal
 
         xc = keep.tile([P, NT, NG * P], U32, name="xc", align_bytes=64)
         xs = keep.tile([P, NT, NG * P], U8, name="xs", align_bytes=64)
+        xts = []
+        xgs = []
 
-        def x_prep(a):
+        def x_transpose(a):
             words = x_all[:, a, :].bitcast(F32)
             xt = psum.tile([P, NG, 2, P], F32, name="xt", tag="bank")
             for g in range(NG):
                 for u in range(2):
                     nc.tensor.transpose(xt[:, g, u, :], words[:, 256 * g + u : 256 * (g + 1) : 2], ident[:])
-            xg = work.tile([P, NG * P * 4], BF16, name="xg", align_bytes=64)
-            dst = xg[:].bitcast(F32).rearrange("p (g r u) -> p g r u", g=NG, u=2)
-            src = xt[:].rearrange("p g u r -> p g r u")
-            if X_COPY_ON_VECTOR:
-                nc.vector.tensor_copy(out=dst, in_=src)
+            xts.append(xt)
+
+        def x_copy(a):
+            if a % 2 == 0:
+                xg_new = xwork.tile([P, 2, NG * P * 4], BF16, name="xg", align_bytes=64)
+                xgs.append(xg_new)
+            xg = xgs[a // 2]
+            dst = xg[:, a % 2, :].bitcast(F32).rearrange("p (g r u) -> p g r u", g=NG, u=2)
+            src = xts[a][:].rearrange("p g u r -> p g r u")
+            nc.scalar.copy(out=dst, in_=src)
+
+        def x_quant(pair):
+            nc.vector.quantize_mx(
+                out=xc[:, 2 * pair : 2 * pair + 2, :].rearrange("p a c -> p (a c)").bitcast(FP8X4),
+                scales=xs[:, 2 * pair : 2 * pair + 2, :].rearrange("p a c -> p (a c)"),
+                in_=xgs[pair][:].rearrange("p a c -> p (a c)"),
+            )
+
+        wide = [keep.tile([P, 4, HW], BF16, name="wide%d" % u) for u in range(4)]
+        wcodes = keep.tile([P, NG * 6 * BANK], U32, name="wcodes", align_bytes=64)
+        wscl = keep.tile([P, NG * 6 * BANK], U8, name="wscl", align_bytes=64)
+
+        def chunk(g, y, half):
+            c0 = ((g * 3 + y) * 2 + half) * BANK
+            return slice(c0, c0 + BANK)
+
+        def widen(u, t):
+            half, g = UNITS[u]
+            src = wbytes[g][:, t, half * HW : (half + 1) * HW].bitcast(FP8)
+            if (u, t) in WIDEN_ON_VECTOR:
+                nc.vector.tensor_scalar(out=wide[u][:, t, :], in0=src, scalar1=wsc[:, g, t : t + 1], scalar2=None, op0=ALU.mult)
             else:
-                nc.scalar.copy(out=dst, in_=src)
-            nc.vector.quantize_mx(out=xc[:, a, :].bitcast(FP8X4), scales=xs[:, a, :], in_=xg[:])
+                nc.scalar.activation(out=wide[u][:, t, :], in_=src, func=ACT.Copy, scale=wsc[:, g, t : t + 1])
 
-        wide = [keep.tile([P, NG, 4, QW], BF16, name="wide%d" % qq) for qq in range(NQ)]
-        wcodes = keep.tile([P, NQ, NG * QW], U32, name="wcodes", align_bytes=64)
-        wscl = keep.tile([P, NQ, NG * QW], U8, name="wscl", align_bytes=64)
+        def interleave(u, y):
+            grouped = work.tile([P, BANK * 4], BF16, name="grouped", align_bytes=64)
+            nc.vector.tensor_copy(
+                out=grouped[:].rearrange("p (h d t) -> p h d t", h=4, d=DH, t=4),
+                in_=wide[u][:].rearrange("p t (h y d) -> p y h d t", h=4, y=3, d=DH)[:, y],
+            )
+            return grouped
 
-        def widen(qq, g, t):
-            src = wbytes[g][:, t, qq * QW : (qq + 1) * QW].bitcast(FP8)
-            if (qq, g, t) in WIDEN_ON_VECTOR:
-                nc.vector.tensor_scalar(
-                    out=wide[qq][:, g, t, :], in0=src, scalar1=wsc[:, g, t : t + 1], scalar2=None, op0=ALU.mult
-                )
-            else:
-                nc.scalar.activation(out=wide[qq][:, g, t, :], in_=src, func=ACT.Copy, scale=wsc[:, g, t : t + 1])
+        def w_quant(u, y, grouped):
+            half, g = UNITS[u]
+            cols = chunk(g, y, half)
+            nc.vector.quantize_mx(out=wcodes[:, cols].bitcast(FP8X4), scales=wscl[:, cols], in_=grouped[:])
 
-        def w_quant(qq, g):
-            grouped = work.tile([P, QW * 4], BF16, name="grouped", align_bytes=64)
-            for ty in range(3):
-                nc.vector.tensor_copy(
-                    out=grouped[:, ty * 1024 : (ty + 1) * 1024].rearrange("p (i d t) -> p i d t", i=2, d=DH, t=4),
-                    in_=wide[qq][:, g].rearrange("p t (i y d) -> p y i d t", i=2, y=3, d=DH)[:, ty],
-                )
-            for c0, c1 in ((0, 512), (512, 768)):
-                nc.vector.quantize_mx(
-                    out=wcodes[:, qq, g * QW + c0 : g * QW + c1].bitcast(FP8X4),
-                    scales=wscl[:, qq, g * QW + c0 : g * QW + c1],
-                    in_=grouped[:, 4 * c0 : 4 * c1],
-                )
+        def w_unit(u, fills):
+            gq = interleave(u, 0)
+            gk = interleave(u, 1)
+            w_quant(u, 0, gq)
+            fills[0]()
+            gv = interleave(u, 2)
+            w_quant(u, 1, gk)
+            fills[1]()
+            w_quant(u, 2, gv)
+
+        def nothing():
+            return None
+
+        for a in range(NT):
+            x_transpose(a)
+        for u in range(4):
+            for t in range(4):
+                if (u, t) not in WIDEN_ON_VECTOR:
+                    widen(u, t)
+        for a in range(NT):
+            x_copy(a)
+        tables_on_scalar()
+
+        for t in range(4):
+            if (0, t) in WIDEN_ON_VECTOR:
+                widen(0, t)
+        w_unit(0, (nothing, nothing))
+        w_unit(1, (nothing, nothing))
+        w_unit(2, (nothing, nothing))
+        widen(3, 3)
+        w_unit(3, (lambda: x_quant(0), lambda: x_quant(1)))
+        x_quant(2)
+        x_quant(3)
 
         junk = keep.tile([P, DH], BF16, name="junk")
+        ss_all = keep.tile([P, 2 * NT * 2, 4], F32, name="ss_all")
+        rn_all = keep.tile([P, 2 * NT * 2, 4], F32, name="rn_all")
 
-        def mx(out, a, qq, c0, c1):
+        def mx(a, y, half):
+            acc = psum.tile([P, BANK], F32, name="acc", tag="bank")
             for g in range(NG):
+                cols = chunk(g, y, half)
                 nc.tensor.matmul_mx(
-                    out=out,
+                    out=acc[:],
                     lhsT=xc[:, a, g * P : (g + 1) * P].bitcast(FP8X4),
                     lhsT_scale=xs[:, a, g * P : (g + 1) * P],
-                    rhs=wcodes[:, qq, g * QW + c0 : g * QW + c1].bitcast(FP8X4),
-                    rhs_scale=wscl[:, qq, g * QW + c0 : g * QW + c1],
+                    rhs=wcodes[:, cols].bitcast(FP8X4),
+                    rhs_scale=wscl[:, cols],
                     start=(g == 0),
                     stop=(g == NG - 1),
                 )
+            return acc
 
-        def step(j, qq, fill_scalar, fill_middle, fill_vector):
-            a0 = 2 * j
-            accs = []
-            for e in range(2):
-                acc = psum.tile([P, BANK], F32, name="acc", tag="bank")
-                mx(acc[:], a0 + e, qq, 0, BANK)
-                accs.append(acc)
-            accv = psum.tile([P, 2, 256], F32, name="accv", tag="bank")
-            for e in range(2):
-                mx(accv[:, e, :], a0 + e, qq, BANK, QW)
-            rns = []
-            for e in range(2):
-                ss = stage.tile([P, 4], F32, name="ss")
-                for i in range(4):
+        item = 0
+        for half in range(2):
+            for a in range(NT):
+                rows = slice(a * P, (a + 1) * P)
+                cols = slice(half * BANK, (half + 1) * BANK)
+                accv = mx(a, 2, half)
+                ov = store.tile([P, BANK], F32, name="ov")
+                nc.scalar.copy(out=ov[:], in_=accv[:])
+                nc.sync.dma_start(out=outs[2][rows, cols], in_=ov[:])
+                for y in range(2):
+                    acc = mx(a, y, half)
+                    for i in range(4):
+                        nc.scalar.activation(
+                            out=junk[:],
+                            in_=acc[:, i * DH : (i + 1) * DH],
+                            func=ACT.Square,
+                            accum_out=ss_all[:, item, i : i + 1],
+                        )
                     nc.scalar.activation(
-                        out=junk[:], in_=accs[e][:, i * DH : (i + 1) * DH], func=ACT.Square, accum_out=ss[:, i : i + 1]
+                        out=rn_all[:, item, :], in_=ss_all[:, item, :], func=ACT.Abs_reciprocal_sqrt, scale=1.0 / DH, bias=EPS
                     )
-                rt = stage.tile([P, 4], F32, name="rt")
-                nc.scalar.activation(out=rt[:], in_=ss[:], func=ACT.Sqrt, scale=1.0 / DH, bias=EPS)
-                rn = stage.tile([P, 4], F32, name="rn")
-                nc.vector.reciprocal(out=rn[:], in_=rt[:])
-                rns.append(rn)
-            rows = slice(a0 * P, (a0 + 2) * P)
-            cols = slice(qq * 256, (qq + 1) * 256)
-            ov = store.tile([P, 2, 256], F32, name="ov")
-            nc.scalar.copy(out=ov[:], in_=accv[:])
-            nc.sync.dma_start(out=outs[2][rows, cols].rearrange("(e p) c -> p e c", p=P), in_=ov[:])
-            fill_scalar()
-            fill_middle()
-            o = store.tile([P, 2, BANK], F32, name="o")
-            for e in range(2):
-                pq = stage.tile([P, 4, 4 * HALF], F32, name="pq")
-                for i in range(4):
-                    nc.vector.scalar_tensor_tensor(
-                        out=pq[:, i, :].rearrange("p (r c) -> p r c", r=2),
-                        in0=accs[e][:, i * DH : (i + 1) * DH].unsqueeze(1).to_broadcast([P, 2, DH]),
-                        scalar=rns[e][:, i : i + 1],
-                        in1=cs[:, a0 + e].rearrange("p (r b) j -> p r (b j)", r=2),
-                        op0=ALU.mult,
-                        op1=ALU.mult,
+                    pq = stage.tile([P, 4, 4 * HALF], F32, name="pq")
+                    for i in range(4):
+                        nc.vector.scalar_tensor_tensor(
+                            out=pq[:, i, :].rearrange("p (r c) -> p r c", r=2),
+                            in0=acc[:, i * DH : (i + 1) * DH].unsqueeze(1).to_broadcast([P, 2, DH]),
+                            scalar=rn_all[:, item, i : i + 1],
+                            in1=cs[:, a].rearrange("p (r b) j -> p r (b j)", r=2),
+                            op0=ALU.mult,
+                            op1=ALU.mult,
+                        )
+                    pairs = pq[:].rearrange("p i (h b j) -> p (i h) b j", h=2, b=2)
+                    o = store.tile([P, BANK], F32, name="o")
+                    nc.gpsimd.tensor_tensor(
+                        out=o[:].rearrange("p (m j) -> p m j", j=HALF),
+                        in0=pairs[:, :, 0, :],
+                        in1=pairs[:, :, 1, :],
+                        op=ALU.add,
                     )
-                pairs = pq[:].rearrange("p i (h b j) -> p (i h) b j", h=2, b=2)
-                eng = nc.gpsimd if (POOL_ADDS and e == 0) else nc.vector
-                eng.tensor_tensor(
-                    out=o[:, e, :].rearrange("p (m j) -> p m j", j=HALF),
-                    in0=pairs[:, :, 0, :],
-                    in1=pairs[:, :, 1, :],
-                    op=ALU.add,
-                )
-            for ty in range(2):
-                nc.sync.dma_start(
-                    out=outs[ty][rows, cols].rearrange("(e p) c -> p e c", p=P), in_=o[:, :, ty * 256 : (ty + 1) * 256]
-                )
-            fill_vector()
-
-        for t in range(4):
-            widen(0, 0, t)
-        x_prep(0)
-        x_prep(1)
-        w_quant(0, 0)
-        for t in range(4):
-            widen(0, 1, t)
-        tables_on_scalar()
-        w_quant(0, 1)
-
-        todo = [(qq, g, t) for qq in range(1, NQ) for g in range(NG) for t in range(4)]
-        done = [0]
-
-        def fill_scalar_for(s):
-            def fill():
-                for k in range(WIDEN_PER_STEP[s]):
-                    widen(*todo[done[0]])
-                    done[0] += 1
-
-            return fill
-
-        def fill_middle_for(s):
-            def fill():
-                if s < 3:
-                    x_prep(2 * s + 2)
-                    x_prep(2 * s + 3)
-
-            return fill
-
-        def fill_vector_for(s):
-            def fill():
-                if s // 4 < NQ - 1 and s % 4 in QUANT_AFTER:
-                    w_quant(s // 4 + 1, QUANT_AFTER.index(s % 4))
-
-            return fill
-
-        for s in range(4 * NQ):
-            step(s % 4, s // 4, fill_scalar_for(s), fill_middle_for(s), fill_vector_for(s))
+                    nc.sync.dma_start(out=outs[y][rows, cols], in_=o[:])
+                    item += 1

@@ -229,7 +229,8 @@ def tile_mixerdiffattention_pa_kernel(tc, hidden_states, W_qkv_bytes, W_qkv_scal
         x_quant(2)
         x_quant(3)
 
-        junk = keep.tile([P, DH], BF16, name="junk")
+        NJ = 8
+        junk = keep.tile([P, NJ, DH], BF16, name="junk")
         ss_all = keep.tile([P, 2 * NT * 2, 4], F32, name="ss_all")
         rn_all = keep.tile([P, 2 * NT * 2, 4], F32, name="rn_all")
 
@@ -248,33 +249,40 @@ def tile_mixerdiffattention_pa_kernel(tc, hidden_states, W_qkv_bytes, W_qkv_scal
                 )
             return acc
 
-        item = 0
+        group = 0
         for half in range(2):
             for a in range(NT):
                 rows = slice(a * P, (a + 1) * P)
                 cols = slice(half * BANK, (half + 1) * BANK)
                 accv = mx(a, 2, half)
-                ov = store.tile([P, BANK], F32, name="ov")
-                nc.scalar.copy(out=ov[:], in_=accv[:])
-                nc.sync.dma_start(out=outs[2][rows, cols], in_=ov[:])
+                accs = []
                 for y in range(2):
                     acc = mx(a, y, half)
                     for i in range(4):
                         nc.scalar.activation(
-                            out=junk[:],
+                            out=junk[:, (4 * y + i) % NJ, :],
                             in_=acc[:, i * DH : (i + 1) * DH],
                             func=ACT.Square,
-                            accum_out=ss_all[:, item, i : i + 1],
+                            accum_out=ss_all[:, 2 * group + y, i : i + 1],
                         )
-                    nc.scalar.activation(
-                        out=rn_all[:, item, :], in_=ss_all[:, item, :], func=ACT.Abs_reciprocal_sqrt, scale=1.0 / DH, bias=EPS
-                    )
+                    accs.append(acc)
+                ov = store.tile([P, BANK], F32, name="ov")
+                nc.scalar.copy(out=ov[:], in_=accv[:])
+                nc.sync.dma_start(out=outs[2][rows, cols], in_=ov[:])
+                nc.scalar.activation(
+                    out=rn_all[:, 2 * group : 2 * group + 2, :],
+                    in_=ss_all[:, 2 * group : 2 * group + 2, :],
+                    func=ACT.Abs_reciprocal_sqrt,
+                    scale=1.0 / DH,
+                    bias=EPS,
+                )
+                for y in range(2):
                     pq = stage.tile([P, 4, 4 * HALF], F32, name="pq")
                     for i in range(4):
                         nc.vector.scalar_tensor_tensor(
                             out=pq[:, i, :].rearrange("p (r c) -> p r c", r=2),
-                            in0=acc[:, i * DH : (i + 1) * DH].unsqueeze(1).to_broadcast([P, 2, DH]),
-                            scalar=rn_all[:, item, i : i + 1],
+                            in0=accs[y][:, i * DH : (i + 1) * DH].unsqueeze(1).to_broadcast([P, 2, DH]),
+                            scalar=rn_all[:, 2 * group + y, i : i + 1],
                             in1=cs[:, a].rearrange("p (r b) j -> p r (b j)", r=2),
                             op0=ALU.mult,
                             op1=ALU.mult,
@@ -288,4 +296,4 @@ def tile_mixerdiffattention_pa_kernel(tc, hidden_states, W_qkv_bytes, W_qkv_scal
                         op=ALU.add,
                     )
                     nc.sync.dma_start(out=outs[y][rows, cols], in_=o[:])
-                    item += 1
+                group += 1

@@ -35,6 +35,7 @@ MAGIC = 12582912.0
 
 UNITS = ((0, 0), (0, 1), (1, 0), (1, 1))
 WIDEN_ON_VECTOR = ((0, 1), (0, 2), (0, 3), (3, 3))
+TAIL_GROUPS_ON_VECTOR = 1
 
 
 def tile_mixerdiffattention_pa_kernel(tc, hidden_states, W_qkv_bytes, W_qkv_scale, out_0, out_1, out_2):
@@ -74,7 +75,8 @@ def tile_mixerdiffattention_pa_kernel(tc, hidden_states, W_qkv_bytes, W_qkv_scal
                 in_=x_dram[a0 * P : (a0 + n) * P, :].rearrange("(a p) k -> p a k", p=P),
             )
 
-        load_w(0)
+        for t in range(4):
+            nc.sync.dma_start(out=wbytes[0][:, t, 0:HW], in_=w_dram[0][:, t, 0:HW])
         load_w(1)
         load_x(0, 2)
         load_x(2, 2)
@@ -86,20 +88,20 @@ def tile_mixerdiffattention_pa_kernel(tc, hidden_states, W_qkv_bytes, W_qkv_scal
         warm = keep.tile([P, 1], F32, name="warm")
         nc.vector.memset(warm[:], 0.0)
         nc.scalar.activation(out=warm[:], in_=warm[:], func=ACT.Sin)
+        ident = keep.tile([P, P], F32, name="ident")
+        make_identity(nc, ident[:])
         freq = keep.tile([P, HALF], F32, name="freq")
-        nc.vector.memset(freq[:, 0:1], 1.0)
+        nc.gpsimd.memset(freq[:, 0:1], 1.0)
         for b in range(6):
             n = 2**b
-            nc.vector.tensor_scalar(
+            nc.gpsimd.tensor_scalar(
                 out=freq[:, n : 2 * n], in0=freq[:, 0:n], scalar1=10000.0 ** (-n / 64.0), scalar2=None, op0=ALU.mult
             )
         tpos = keep.tile([P, NT], F32, name="tpos")
         nc.gpsimd.iota(tpos[:], pattern=[[P, NT]], base=0, channel_multiplier=1, allow_small_or_imprecise_dtypes=True)
-        ident = keep.tile([P, P], F32, name="ident")
-        make_identity(nc, ident[:])
         NA = NT * HALF
         theta = keep.tile([P, NT, HALF], F32, name="theta")
-        nc.vector.tensor_tensor(
+        nc.gpsimd.tensor_tensor(
             out=theta[:],
             in0=freq[:].unsqueeze(1).to_broadcast([P, NT, HALF]),
             in1=tpos[:].unsqueeze(2).to_broadcast([P, NT, HALF]),
@@ -107,28 +109,50 @@ def tile_mixerdiffattention_pa_kernel(tc, hidden_states, W_qkv_bytes, W_qkv_scal
         )
         theta_f = theta[:].rearrange("p a j -> p (a j)")
         turns = keep.tile([P, NA], F32, name="turns")
-        nc.vector.tensor_scalar(
-            out=turns[:], in0=theta_f, scalar1=1.0 / TWO_PI, scalar2=-0.125, op0=ALU.mult, op1=ALU.add
-        )
         whole = keep.tile([P, NA], I32, name="whole")
-        nc.vector.tensor_scalar(out=whole[:], in0=turns[:], scalar1=MAGIC, scalar2=MAGIC, op0=ALU.add, op1=ALU.subtract)
+        rest0 = keep.tile([P, NA], F32, name="rest0")
         rest = keep.tile([P, NA], F32, name="rest")
-        nc.vector.scalar_tensor_tensor(out=rest[:], in0=whole[:], scalar=-C1, in1=theta_f, op0=ALU.mult, op1=ALU.add)
-        nc.vector.scalar_tensor_tensor(out=rest[:], in0=whole[:], scalar=-C2, in1=rest[:], op0=ALU.mult, op1=ALU.add)
         shifted = keep.tile([P, NA], F32, name="shifted")
-        nc.vector.tensor_scalar(out=shifted[:], in0=rest[:], scalar1=-0.5 * math.pi, scalar2=None, op0=ALU.add)
         mag = keep.tile([P, 2, NT, HALF], F32, name="mag")
-        nc.vector.scalar_tensor_tensor(
-            out=mag[:, 0].rearrange("p a j -> p (a j)"), in0=rest[:], scalar=-1.0, in1=rest[:], op0=ALU.mult, op1=ALU.max
-        )
-        nc.vector.scalar_tensor_tensor(
-            out=mag[:, 1].rearrange("p a j -> p (a j)"),
-            in0=shifted[:],
-            scalar=-1.0,
-            in1=shifted[:],
-            op0=ALU.mult,
-            op1=ALU.max,
-        )
+
+        def table_step(k):
+            if k == 0:
+                nc.vector.tensor_scalar(
+                    out=turns[:], in0=theta_f, scalar1=1.0 / TWO_PI, scalar2=-0.125, op0=ALU.mult, op1=ALU.add
+                )
+            elif k == 1:
+                nc.vector.tensor_scalar(
+                    out=whole[:], in0=turns[:], scalar1=MAGIC, scalar2=MAGIC, op0=ALU.add, op1=ALU.subtract
+                )
+            elif k == 2:
+                nc.vector.scalar_tensor_tensor(
+                    out=rest0[:], in0=whole[:], scalar=-C1, in1=theta_f, op0=ALU.mult, op1=ALU.add
+                )
+            elif k == 3:
+                nc.vector.scalar_tensor_tensor(
+                    out=rest[:], in0=whole[:], scalar=-C2, in1=rest0[:], op0=ALU.mult, op1=ALU.add
+                )
+            elif k == 4:
+                nc.vector.tensor_scalar(out=shifted[:], in0=rest[:], scalar1=-0.5 * math.pi, scalar2=None, op0=ALU.add)
+            elif k == 5:
+                nc.vector.scalar_tensor_tensor(
+                    out=mag[:, 0].rearrange("p a j -> p (a j)"),
+                    in0=rest[:],
+                    scalar=-1.0,
+                    in1=rest[:],
+                    op0=ALU.mult,
+                    op1=ALU.max,
+                )
+            else:
+                nc.vector.scalar_tensor_tensor(
+                    out=mag[:, 1].rearrange("p a j -> p (a j)"),
+                    in0=shifted[:],
+                    scalar=-1.0,
+                    in1=shifted[:],
+                    op0=ALU.mult,
+                    op1=ALU.max,
+                )
+
         cs = keep.tile([P, NT, 4, HALF], F32, name="cs")
 
         def tables_on_scalar():
@@ -197,12 +221,14 @@ def tile_mixerdiffattention_pa_kernel(tc, hidden_states, W_qkv_bytes, W_qkv_scal
 
         def w_unit(u, fills):
             gq = interleave(u, 0)
-            gk = interleave(u, 1)
-            w_quant(u, 0, gq)
             fills[0]()
-            gv = interleave(u, 2)
-            w_quant(u, 1, gk)
+            gk = interleave(u, 1)
             fills[1]()
+            w_quant(u, 0, gq)
+            gv = interleave(u, 2)
+            fills[2]()
+            w_quant(u, 1, gk)
+            fills[3]()
             w_quant(u, 2, gv)
 
         def nothing():
@@ -216,17 +242,16 @@ def tile_mixerdiffattention_pa_kernel(tc, hidden_states, W_qkv_bytes, W_qkv_scal
                     widen(u, t)
         for a in range(NT):
             x_copy(a)
-        tables_on_scalar()
 
         for t in range(4):
             if (0, t) in WIDEN_ON_VECTOR:
                 widen(0, t)
-        w_unit(0, (nothing, nothing))
-        w_unit(1, (nothing, nothing))
-        w_unit(2, (nothing, nothing))
+        w_unit(0, (lambda: table_step(0), lambda: table_step(1), lambda: table_step(2), lambda: table_step(3)))
+        w_unit(1, (lambda: table_step(4), lambda: table_step(5), lambda: table_step(6), nothing))
+        tables_on_scalar()
+        w_unit(2, (nothing, nothing, nothing, nothing))
         widen(3, 3)
-        w_unit(3, (lambda: x_quant(0), lambda: x_quant(1)))
-        x_quant(2)
+        w_unit(3, (nothing, lambda: x_quant(0), lambda: x_quant(1), lambda: x_quant(2)))
         x_quant(3)
 
         NJ = 8
@@ -276,6 +301,7 @@ def tile_mixerdiffattention_pa_kernel(tc, hidden_states, W_qkv_bytes, W_qkv_scal
                     scale=1.0 / DH,
                     bias=EPS,
                 )
+                pqs = []
                 for y in range(2):
                     pq = stage.tile([P, 4, 4 * HALF], F32, name="pq")
                     for i in range(4):
@@ -287,9 +313,12 @@ def tile_mixerdiffattention_pa_kernel(tc, hidden_states, W_qkv_bytes, W_qkv_scal
                             op0=ALU.mult,
                             op1=ALU.mult,
                         )
-                    pairs = pq[:].rearrange("p i (h b j) -> p (i h) b j", h=2, b=2)
+                    pqs.append(pq)
+                for y in range(2):
+                    pairs = pqs[y][:].rearrange("p i (h b j) -> p (i h) b j", h=2, b=2)
                     o = store.tile([P, BANK], F32, name="o")
-                    nc.gpsimd.tensor_tensor(
+                    adder = nc.vector if group >= 2 * NT - TAIL_GROUPS_ON_VECTOR else nc.gpsimd
+                    adder.tensor_tensor(
                         out=o[:].rearrange("p (m j) -> p m j", j=HALF),
                         in0=pairs[:, :, 0, :],
                         in1=pairs[:, :, 1, :],

@@ -35,7 +35,7 @@ MAGIC = 12582912.0
 
 UNITS = ((0, 0), (0, 1), (1, 0), (1, 1))
 WIDEN_ON_VECTOR = ((0, 1), (0, 2), (0, 3), (3, 3))
-TAIL_GROUPS_ON_VECTOR = 1
+TAIL_GROUPS_ON_VECTOR = 2
 
 
 def tile_mixerdiffattention_pa_kernel(tc, hidden_states, W_qkv_bytes, W_qkv_scale, out_0, out_1, out_2):
@@ -51,10 +51,9 @@ def tile_mixerdiffattention_pa_kernel(tc, hidden_states, W_qkv_bytes, W_qkv_scal
 
     with ExitStack() as ctx:
         keep = ctx.enter_context(tc.tile_pool(name="keep", bufs=1))
-        work = ctx.enter_context(tc.tile_pool(name="work", bufs=3))
+        work = ctx.enter_context(tc.tile_pool(name="work", bufs=4))
         xwork = ctx.enter_context(tc.tile_pool(name="xwork", bufs=4))
-        stage = ctx.enter_context(tc.tile_pool(name="stage", bufs=4))
-        store = ctx.enter_context(tc.tile_pool(name="store", bufs=6))
+        store = ctx.enter_context(tc.tile_pool(name="store", bufs=4))
         psum = ctx.enter_context(tc.psum_pool(name="psum", bufs=8))
         ctx.enter_context(tc.manual_schedule())
 
@@ -207,7 +206,7 @@ def tile_mixerdiffattention_pa_kernel(tc, hidden_states, W_qkv_bytes, W_qkv_scal
                 nc.scalar.activation(out=wide[u][:, t, :], in_=src, func=ACT.Copy, scale=wsc[:, g, t : t + 1])
 
         def interleave(u, y):
-            grouped = work.tile([P, BANK * 4], BF16, name="grouped", align_bytes=64)
+            grouped = work.tile([P, BANK * 4], BF16, name="grouped", tag="slab", align_bytes=64)
             nc.vector.tensor_copy(
                 out=grouped[:].rearrange("p (h d t) -> p h d t", h=4, d=DH, t=4),
                 in_=wide[u][:].rearrange("p t (h y d) -> p y h d t", h=4, y=3, d=DH)[:, y],
@@ -301,28 +300,26 @@ def tile_mixerdiffattention_pa_kernel(tc, hidden_states, W_qkv_bytes, W_qkv_scal
                     scale=1.0 / DH,
                     bias=EPS,
                 )
-                pqs = []
+                pq = work.tile([P, 8, 4 * HALF], F32, name="pq", tag="slab", align_bytes=64)
                 for y in range(2):
-                    pq = stage.tile([P, 4, 4 * HALF], F32, name="pq")
                     for i in range(4):
                         nc.vector.scalar_tensor_tensor(
-                            out=pq[:, i, :].rearrange("p (r c) -> p r c", r=2),
+                            out=pq[:, 4 * y + i, :].rearrange("p (r c) -> p r c", r=2),
                             in0=accs[y][:, i * DH : (i + 1) * DH].unsqueeze(1).to_broadcast([P, 2, DH]),
                             scalar=rn_all[:, 2 * group + y, i : i + 1],
                             in1=cs[:, a].rearrange("p (r b) j -> p r (b j)", r=2),
                             op0=ALU.mult,
                             op1=ALU.mult,
                         )
-                    pqs.append(pq)
+                pairs = pq[:].rearrange("p i (h b j) -> p (i h) b j", h=2, b=2)
+                o = store.tile([P, 2, BANK], F32, name="o")
+                adder = nc.vector if group >= 2 * NT - TAIL_GROUPS_ON_VECTOR else nc.gpsimd
+                adder.tensor_tensor(
+                    out=o[:].rearrange("p y (m j) -> p (y m) j", j=HALF),
+                    in0=pairs[:, :, 0, :],
+                    in1=pairs[:, :, 1, :],
+                    op=ALU.add,
+                )
                 for y in range(2):
-                    pairs = pqs[y][:].rearrange("p i (h b j) -> p (i h) b j", h=2, b=2)
-                    o = store.tile([P, BANK], F32, name="o")
-                    adder = nc.vector if group >= 2 * NT - TAIL_GROUPS_ON_VECTOR else nc.gpsimd
-                    adder.tensor_tensor(
-                        out=o[:].rearrange("p (m j) -> p m j", j=HALF),
-                        in0=pairs[:, :, 0, :],
-                        in1=pairs[:, :, 1, :],
-                        op=ALU.add,
-                    )
-                    nc.sync.dma_start(out=outs[y][rows, cols], in_=o[:])
+                    nc.sync.dma_start(out=outs[y][rows, cols], in_=o[:, y, :])
                 group += 1

@@ -208,8 +208,8 @@ def tile_mixerdiffattention_pa_kernel(tc, hidden_states, W_qkv_bytes, W_qkv_scal
         def interleave(u, y):
             grouped = work.tile([P, BANK * 4], BF16, name="grouped", tag="slab", align_bytes=64)
             nc.vector.tensor_copy(
-                out=grouped[:].rearrange("p (h d t) -> p h d t", h=4, d=DH, t=4),
-                in_=wide[u][:].rearrange("p t (h y d) -> p y h d t", h=4, y=3, d=DH)[:, y],
+                out=grouped[:].rearrange("p (h c i t) -> p h c t i", h=4, c=DH // 4, i=4, t=4),
+                in_=wide[u][:].rearrange("p t (h y c i) -> p y h c t i", h=4, y=3, c=DH // 4, i=4)[:, y],
             )
             return grouped
 

@@ -34,7 +34,7 @@ C2 = TWO_PI - C1
 MAGIC = 12582912.0
 
 UNITS = ((0, 0), (0, 1), (1, 0), (1, 1))
-WIDEN_ON_VECTOR = ((0, 1), (0, 2), (0, 3), (3, 3))
+WIDEN_ON_VECTOR = ((0, 1), (0, 2), (0, 3), (2, 3), (3, 3))
 TAIL_GROUPS_ON_VECTOR = 2
 
 
@@ -87,20 +87,20 @@ def tile_mixerdiffattention_pa_kernel(tc, hidden_states, W_qkv_bytes, W_qkv_scal
         warm = keep.tile([P, 1], F32, name="warm")
         nc.vector.memset(warm[:], 0.0)
         nc.scalar.activation(out=warm[:], in_=warm[:], func=ACT.Sin)
+        tpos = keep.tile([P, NT], F32, name="tpos")
+        nc.gpsimd.iota(tpos[:], pattern=[[P, NT]], base=0, channel_multiplier=1, allow_small_or_imprecise_dtypes=True)
         ident = keep.tile([P, P], F32, name="ident")
         make_identity(nc, ident[:])
         freq = keep.tile([P, HALF], F32, name="freq")
-        nc.gpsimd.memset(freq[:, 0:1], 1.0)
+        nc.vector.memset(freq[:, 0:1], 1.0)
         for b in range(6):
             n = 2**b
-            nc.gpsimd.tensor_scalar(
+            nc.vector.tensor_scalar(
                 out=freq[:, n : 2 * n], in0=freq[:, 0:n], scalar1=10000.0 ** (-n / 64.0), scalar2=None, op0=ALU.mult
             )
-        tpos = keep.tile([P, NT], F32, name="tpos")
-        nc.gpsimd.iota(tpos[:], pattern=[[P, NT]], base=0, channel_multiplier=1, allow_small_or_imprecise_dtypes=True)
         NA = NT * HALF
         theta = keep.tile([P, NT, HALF], F32, name="theta")
-        nc.gpsimd.tensor_tensor(
+        nc.vector.tensor_tensor(
             out=theta[:],
             in0=freq[:].unsqueeze(1).to_broadcast([P, NT, HALF]),
             in1=tpos[:].unsqueeze(2).to_broadcast([P, NT, HALF]),
@@ -220,14 +220,18 @@ def tile_mixerdiffattention_pa_kernel(tc, hidden_states, W_qkv_bytes, W_qkv_scal
 
         def w_unit(u, fills):
             gq = interleave(u, 0)
-            fills[0]()
+            for f in fills[0]:
+                f()
             gk = interleave(u, 1)
-            fills[1]()
+            for f in fills[1]:
+                f()
             w_quant(u, 0, gq)
             gv = interleave(u, 2)
-            fills[2]()
+            for f in fills[2]:
+                f()
             w_quant(u, 1, gk)
-            fills[3]()
+            for f in fills[3]:
+                f()
             w_quant(u, 2, gv)
 
         def nothing():
@@ -242,15 +246,23 @@ def tile_mixerdiffattention_pa_kernel(tc, hidden_states, W_qkv_bytes, W_qkv_scal
         for a in range(NT):
             x_copy(a)
 
-        for t in range(4):
-            if (0, t) in WIDEN_ON_VECTOR:
-                widen(0, t)
-        w_unit(0, (lambda: table_step(0), lambda: table_step(1), lambda: table_step(2), lambda: table_step(3)))
-        w_unit(1, (lambda: table_step(4), lambda: table_step(5), lambda: table_step(6), nothing))
+        def tab(k):
+            return lambda: table_step(k)
+
+        def wid(u, t):
+            return lambda: widen(u, t)
+
+        def xq(pair):
+            return lambda: x_quant(pair)
+
+        widen(0, 1)
+        widen(0, 2)
+        widen(0, 3)
+        w_unit(0, ([tab(0)], [tab(1)], [tab(2)], [tab(3)]))
+        w_unit(1, ([tab(4), wid(2, 3)], [tab(5)], [tab(6)], []))
         tables_on_scalar()
-        w_unit(2, (nothing, nothing, nothing, nothing))
-        widen(3, 3)
-        w_unit(3, (nothing, lambda: x_quant(0), lambda: x_quant(1), lambda: x_quant(2)))
+        w_unit(2, ([wid(3, 3)], [], [], []))
+        w_unit(3, ([], [xq(0)], [xq(1)], [xq(2)]))
         x_quant(3)
 
         NJ = 8
@@ -290,12 +302,17 @@ def tile_mixerdiffattention_pa_kernel(tc, hidden_states, W_qkv_bytes, W_qkv_scal
                             accum_out=ss_all[:, 2 * group + y, i : i + 1],
                         )
                     accs.append(acc)
+                    if group == 0 and y == 0:
+                        nc.scalar.activation(
+                            out=rn_all[:, 0, :], in_=ss_all[:, 0, :], func=ACT.Abs_reciprocal_sqrt, scale=1.0 / DH, bias=EPS
+                        )
                 ov = store.tile([P, BANK], F32, name="ov")
                 nc.scalar.copy(out=ov[:], in_=accv[:])
                 nc.sync.dma_start(out=outs[2][rows, cols], in_=ov[:])
+                first = 2 * group + (1 if group == 0 else 0)
                 nc.scalar.activation(
-                    out=rn_all[:, 2 * group : 2 * group + 2, :],
-                    in_=ss_all[:, 2 * group : 2 * group + 2, :],
+                    out=rn_all[:, first : 2 * group + 2, :],
+                    in_=ss_all[:, first : 2 * group + 2, :],
                     func=ACT.Abs_reciprocal_sqrt,
                     scale=1.0 / DH,
                     bias=EPS,

@@ -34,8 +34,8 @@ C2 = TWO_PI - C1
 MAGIC = 12582912.0
 
 UNITS = ((0, 0), (0, 1), (1, 0), (1, 1))
-WIDEN_ON_VECTOR = ((0, 1), (0, 2), (0, 3), (2, 3), (3, 3))
-TAIL_GROUPS_ON_VECTOR = 2
+WIDEN_ON_VECTOR = ((0, 1), (0, 2), (0, 3), (1, 3), (2, 3), (3, 3))
+TAIL_GROUPS_ON_VECTOR = 1
 
 
 def tile_mixerdiffattention_pa_kernel(tc, hidden_states, W_qkv_bytes, W_qkv_scale, out_0, out_1, out_2):
@@ -155,6 +155,10 @@ def tile_mixerdiffattention_pa_kernel(tc, hidden_states, W_qkv_bytes, W_qkv_scal
         cs = keep.tile([P, NT, 4, HALF], F32, name="cs")
 
         def tables_on_scalar():
+            nc.scalar.activation(out=mag[:, 0].rearrange("p a j -> p (a j)"), in_=rest[:], func=ACT.Abs)
+            nc.scalar.activation(
+                out=mag[:, 1].rearrange("p a j -> p (a j)"), in_=rest[:], func=ACT.Abs, bias=-0.5 * math.pi
+            )
             nc.scalar.activation(out=cs[:, :, 0, :], in_=mag[:, 0], func=ACT.Sin, scale=-1.0, bias=0.5 * math.pi)
             nc.scalar.activation(out=cs[:, :, 3, :], in_=mag[:, 0], func=ACT.Sin, scale=-1.0, bias=0.5 * math.pi)
             nc.scalar.activation(out=cs[:, :, 1, :], in_=mag[:, 1], func=ACT.Sin, scale=-1.0, bias=0.5 * math.pi)
@@ -258,8 +262,8 @@ def tile_mixerdiffattention_pa_kernel(tc, hidden_states, W_qkv_bytes, W_qkv_scal
         widen(0, 1)
         widen(0, 2)
         widen(0, 3)
-        w_unit(0, ([tab(0)], [tab(1)], [tab(2)], [tab(3)]))
-        w_unit(1, ([tab(4), wid(2, 3)], [tab(5)], [tab(6)], []))
+        w_unit(0, ([tab(0), wid(1, 3)], [tab(1)], [tab(2)], [tab(3)]))
+        w_unit(1, ([wid(2, 3)], [], [], []))
         tables_on_scalar()
         w_unit(2, ([wid(3, 3)], [], [], []))
         w_unit(3, ([], [xq(0)], [xq(1)], [xq(2)]))
@@ -330,13 +334,22 @@ def tile_mixerdiffattention_pa_kernel(tc, hidden_states, W_qkv_bytes, W_qkv_scal
                         )
                 pairs = pq[:].rearrange("p i (h b j) -> p (i h) b j", h=2, b=2)
                 o = store.tile([P, 2, BANK], F32, name="o")
-                adder = nc.vector if group >= 2 * NT - TAIL_GROUPS_ON_VECTOR else nc.gpsimd
-                adder.tensor_tensor(
-                    out=o[:].rearrange("p y (m j) -> p (y m) j", j=HALF),
-                    in0=pairs[:, :, 0, :],
-                    in1=pairs[:, :, 1, :],
-                    op=ALU.add,
-                )
-                for y in range(2):
-                    nc.sync.dma_start(out=outs[y][rows, cols], in_=o[:, y, :])
+                if group < 2 * NT - TAIL_GROUPS_ON_VECTOR:
+                    nc.gpsimd.tensor_tensor(
+                        out=o[:].rearrange("p y (m j) -> p (y m) j", j=HALF),
+                        in0=pairs[:, :, 0, :],
+                        in1=pairs[:, :, 1, :],
+                        op=ALU.add,
+                    )
+                    for y in range(2):
+                        nc.sync.dma_start(out=outs[y][rows, cols], in_=o[:, y, :])
+                else:
+                    for y in range(2):
+                        nc.vector.tensor_tensor(
+                            out=o[:, y, :].rearrange("p (m j) -> p m j", j=HALF),
+                            in0=pairs[:, 8 * y : 8 * y + 8, 0, :],
+                            in1=pairs[:, 8 * y : 8 * y + 8, 1, :],
+                            op=ALU.add,
+                        )
+                        nc.sync.dma_start(out=outs[y][rows, cols], in_=o[:, y, :])
                 group += 1

@@ -29,12 +29,10 @@ EPS = 1e-6
 FLOPS = 2 * T * D * NCOL
 
 TWO_PI = 2.0 * math.pi
-C1 = 6.28125
-C2 = TWO_PI - C1
 MAGIC = 12582912.0
 
 UNITS = ((0, 0), (0, 1), (1, 0), (1, 1))
-WIDEN_ON_VECTOR = ((0, 1), (0, 2), (0, 3), (1, 3), (2, 3), (3, 3))
+WIDEN_ON_VECTOR = ((0, 1), (0, 2), (0, 3), (1, 2), (1, 3), (2, 3))
 TAIL_GROUPS_ON_VECTOR = 1
 
 
@@ -91,78 +89,43 @@ def tile_mixerdiffattention_pa_kernel(tc, hidden_states, W_qkv_bytes, W_qkv_scal
         nc.gpsimd.iota(tpos[:], pattern=[[P, NT]], base=0, channel_multiplier=1, allow_small_or_imprecise_dtypes=True)
         ident = keep.tile([P, P], F32, name="ident")
         make_identity(nc, ident[:])
+        one = keep.tile([P, 1], F32, name="one")
+        nc.vector.memset(one[:], 1.0)
         freq = keep.tile([P, HALF], F32, name="freq")
-        nc.vector.memset(freq[:, 0:1], 1.0)
+        nc.vector.tensor_scalar(out=freq[:, 0:1], in0=one[:], scalar1=1.0 / TWO_PI, scalar2=None, op0=ALU.mult)
         for b in range(6):
             n = 2**b
             nc.vector.tensor_scalar(
                 out=freq[:, n : 2 * n], in0=freq[:, 0:n], scalar1=10000.0 ** (-n / 64.0), scalar2=None, op0=ALU.mult
             )
         NA = NT * HALF
-        theta = keep.tile([P, NT, HALF], F32, name="theta")
+        turns = keep.tile([P, NT, HALF], F32, name="turns")
         nc.vector.tensor_tensor(
-            out=theta[:],
+            out=turns[:],
             in0=freq[:].unsqueeze(1).to_broadcast([P, NT, HALF]),
             in1=tpos[:].unsqueeze(2).to_broadcast([P, NT, HALF]),
             op=ALU.mult,
         )
-        theta_f = theta[:].rearrange("p a j -> p (a j)")
-        turns = keep.tile([P, NA], F32, name="turns")
+        turns_f = turns[:].rearrange("p a j -> p (a j)")
         whole = keep.tile([P, NA], I32, name="whole")
-        rest0 = keep.tile([P, NA], F32, name="rest0")
-        rest = keep.tile([P, NA], F32, name="rest")
-        shifted = keep.tile([P, NA], F32, name="shifted")
+        nc.vector.tensor_scalar(out=whole[:], in0=turns_f, scalar1=-0.125, scalar2=MAGIC, op0=ALU.add, op1=ALU.add)
+        back = keep.tile([P, NA], F32, name="back")
+        nc.vector.scalar_tensor_tensor(
+            out=back[:], in0=whole[:], scalar=MAGIC, in1=turns_f, op0=ALU.subtract, op1=ALU.subtract
+        )
         mag = keep.tile([P, 2, NT, HALF], F32, name="mag")
-
-        def table_step(k):
-            if k == 0:
-                nc.vector.tensor_scalar(
-                    out=turns[:], in0=theta_f, scalar1=1.0 / TWO_PI, scalar2=-0.125, op0=ALU.mult, op1=ALU.add
-                )
-            elif k == 1:
-                nc.vector.tensor_scalar(
-                    out=whole[:], in0=turns[:], scalar1=MAGIC, scalar2=MAGIC, op0=ALU.add, op1=ALU.subtract
-                )
-            elif k == 2:
-                nc.vector.scalar_tensor_tensor(
-                    out=rest0[:], in0=whole[:], scalar=-C1, in1=theta_f, op0=ALU.mult, op1=ALU.add
-                )
-            elif k == 3:
-                nc.vector.scalar_tensor_tensor(
-                    out=rest[:], in0=whole[:], scalar=-C2, in1=rest0[:], op0=ALU.mult, op1=ALU.add
-                )
-            elif k == 4:
-                nc.vector.tensor_scalar(out=shifted[:], in0=rest[:], scalar1=-0.5 * math.pi, scalar2=None, op0=ALU.add)
-            elif k == 5:
-                nc.vector.scalar_tensor_tensor(
-                    out=mag[:, 0].rearrange("p a j -> p (a j)"),
-                    in0=rest[:],
-                    scalar=-1.0,
-                    in1=rest[:],
-                    op0=ALU.mult,
-                    op1=ALU.max,
-                )
-            else:
-                nc.vector.scalar_tensor_tensor(
-                    out=mag[:, 1].rearrange("p a j -> p (a j)"),
-                    in0=shifted[:],
-                    scalar=-1.0,
-                    in1=shifted[:],
-                    op0=ALU.mult,
-                    op1=ALU.max,
-                )
-
         cs = keep.tile([P, NT, 4, HALF], F32, name="cs")
 
         def tables_on_scalar():
-            nc.scalar.activation(out=mag[:, 0].rearrange("p a j -> p (a j)"), in_=rest[:], func=ACT.Abs)
-            nc.scalar.activation(
-                out=mag[:, 1].rearrange("p a j -> p (a j)"), in_=rest[:], func=ACT.Abs, bias=-0.5 * math.pi
-            )
-            nc.scalar.activation(out=cs[:, :, 0, :], in_=mag[:, 0], func=ACT.Sin, scale=-1.0, bias=0.5 * math.pi)
-            nc.scalar.activation(out=cs[:, :, 3, :], in_=mag[:, 0], func=ACT.Sin, scale=-1.0, bias=0.5 * math.pi)
-            nc.scalar.activation(out=cs[:, :, 1, :], in_=mag[:, 1], func=ACT.Sin, scale=-1.0, bias=0.5 * math.pi)
-            nc.scalar.activation(out=cs[:, :, 2, :], in_=mag[:, 1], func=ACT.Sin, scale=1.0, bias=-0.5 * math.pi)
+            nc.scalar.activation(out=mag[:, 0].rearrange("p a j -> p (a j)"), in_=back[:], func=ACT.Abs)
+            nc.scalar.activation(out=mag[:, 1].rearrange("p a j -> p (a j)"), in_=back[:], func=ACT.Abs, bias=0.25)
+            nc.scalar.activation(out=cs[:, :, 0, :], in_=mag[:, 0], func=ACT.Sin, scale=-TWO_PI, bias=0.5 * math.pi)
+            nc.scalar.activation(out=cs[:, :, 3, :], in_=mag[:, 0], func=ACT.Sin, scale=-TWO_PI, bias=0.5 * math.pi)
+            nc.scalar.activation(out=cs[:, :, 1, :], in_=mag[:, 1], func=ACT.Sin, scale=-TWO_PI, bias=0.5 * math.pi)
+            nc.scalar.activation(out=cs[:, :, 2, :], in_=mag[:, 1], func=ACT.Sin, scale=TWO_PI, bias=-0.5 * math.pi)
+
+        def main_table():
+            nc.scalar.activation(out=warm[:], in_=mag[:, 1, 0, 0:1], func=ACT.Abs_reciprocal_sqrt, scale=1.0, bias=1.0)
 
         xc = keep.tile([P, NT, NG * P], U32, name="xc", align_bytes=64)
         xs = keep.tile([P, NT, NG * P], U8, name="xs", align_bytes=64)
@@ -243,15 +206,17 @@ def tile_mixerdiffattention_pa_kernel(tc, hidden_states, W_qkv_bytes, W_qkv_scal
 
         for a in range(NT):
             x_transpose(a)
-        for u in range(4):
+        widen(0, 0)
+        tables_on_scalar()
+        for u in range(1, 4):
             for t in range(4):
                 if (u, t) not in WIDEN_ON_VECTOR:
                     widen(u, t)
         for a in range(NT):
             x_copy(a)
-
-        def tab(k):
-            return lambda: table_step(k)
+        main_table()
+        for t in range(1, 4):
+            widen(0, t)
 
         def wid(u, t):
             return lambda: widen(u, t)
@@ -259,13 +224,9 @@ def tile_mixerdiffattention_pa_kernel(tc, hidden_states, W_qkv_bytes, W_qkv_scal
         def xq(pair):
             return lambda: x_quant(pair)
 
-        widen(0, 1)
-        widen(0, 2)
-        widen(0, 3)
-        w_unit(0, ([tab(0), wid(1, 3)], [tab(1)], [tab(2)], [tab(3)]))
+        w_unit(0, ([wid(1, 2)], [wid(1, 3)], [], []))
         w_unit(1, ([wid(2, 3)], [], [], []))
-        tables_on_scalar()
-        w_unit(2, ([wid(3, 3)], [], [], []))
+        w_unit(2, ([], [], [], []))
         w_unit(3, ([], [xq(0)], [xq(1)], [xq(2)]))
         x_quant(3)
 

@@ -32,7 +32,7 @@ TWO_PI = 2.0 * math.pi
 MAGIC = 12582912.0
 
 UNITS = ((0, 0), (0, 1), (1, 0), (1, 1))
-WIDEN_ON_VECTOR = ((0, 1), (0, 2), (0, 3), (1, 2), (1, 3), (2, 3))
+WIDEN_ON_SCALAR = ((0, 0), (1, 0), (3, 0))
 TAIL_GROUPS_ON_VECTOR = 1
 
 
@@ -49,7 +49,8 @@ def tile_mixerdiffattention_pa_kernel(tc, hidden_states, W_qkv_bytes, W_qkv_scal
 
     with ExitStack() as ctx:
         keep = ctx.enter_context(tc.tile_pool(name="keep", bufs=1))
-        work = ctx.enter_context(tc.tile_pool(name="work", bufs=4))
+        big = ctx.enter_context(tc.tile_pool(name="big", bufs=4))
+        work = ctx.enter_context(tc.tile_pool(name="work", bufs=6))
         xwork = ctx.enter_context(tc.tile_pool(name="xwork", bufs=4))
         store = ctx.enter_context(tc.tile_pool(name="store", bufs=4))
         psum = ctx.enter_context(tc.psum_pool(name="psum", bufs=8))
@@ -75,12 +76,12 @@ def tile_mixerdiffattention_pa_kernel(tc, hidden_states, W_qkv_bytes, W_qkv_scal
         for t in range(4):
             nc.sync.dma_start(out=wbytes[0][:, t, 0:HW], in_=w_dram[0][:, t, 0:HW])
         load_w(1)
+        load_w(2)
         load_x(0, 2)
         load_x(2, 2)
-        load_w(2)
+        load_w(3)
         load_x(4, 2)
         load_x(6, 2)
-        load_w(3)
 
         warm = keep.tile([P, 1], F32, name="warm")
         nc.vector.memset(warm[:], 0.0)
@@ -89,6 +90,8 @@ def tile_mixerdiffattention_pa_kernel(tc, hidden_states, W_qkv_bytes, W_qkv_scal
         nc.gpsimd.iota(tpos[:], pattern=[[P, NT]], base=0, channel_multiplier=1, allow_small_or_imprecise_dtypes=True)
         ident = keep.tile([P, P], F32, name="ident")
         make_identity(nc, ident[:])
+        ident16 = keep.tile([P, P], BF16, name="ident16")
+        nc.gpsimd.tensor_scalar(out=ident16[:], in0=ident[:], scalar1=1.0, scalar2=0.0, op0=ALU.mult, op1=ALU.add)
         one = keep.tile([P, 1], F32, name="one")
         nc.vector.memset(one[:], 1.0)
         freq = keep.tile([P, HALF], F32, name="freq")
@@ -156,7 +159,10 @@ def tile_mixerdiffattention_pa_kernel(tc, hidden_states, W_qkv_bytes, W_qkv_scal
                 in_=xgs[pair][:].rearrange("p a c -> p (a c)"),
             )
 
-        wide = [keep.tile([P, 4, HW], BF16, name="wide%d" % u) for u in range(4)]
+        wide = []
+        for u in range(4):
+            wide_u = big.tile([P, 4, HW], BF16, name="wide_u", tag="big")
+            wide.append(wide_u)
         wcodes = keep.tile([P, NG * 6 * BANK], U32, name="wcodes", align_bytes=64)
         wscl = keep.tile([P, NG * 6 * BANK], U8, name="wscl", align_bytes=64)
 
@@ -167,7 +173,7 @@ def tile_mixerdiffattention_pa_kernel(tc, hidden_states, W_qkv_bytes, W_qkv_scal
         def widen(u, t):
             half, g = UNITS[u]
             src = wbytes[g][:, t, half * HW : (half + 1) * HW].bitcast(FP8)
-            if (u, t) in WIDEN_ON_VECTOR:
+            if (u, t) not in WIDEN_ON_SCALAR:
                 nc.vector.tensor_scalar(out=wide[u][:, t, :], in0=src, scalar1=wsc[:, g, t : t + 1], scalar2=None, op0=ALU.mult)
             else:
                 nc.scalar.activation(out=wide[u][:, t, :], in_=src, func=ACT.Copy, scale=wsc[:, g, t : t + 1])
@@ -184,6 +190,32 @@ def tile_mixerdiffattention_pa_kernel(tc, hidden_states, W_qkv_bytes, W_qkv_scal
             half, g = UNITS[u]
             cols = chunk(g, y, half)
             nc.vector.quantize_mx(out=wcodes[:, cols].bitcast(FP8X4), scales=wscl[:, cols], in_=grouped[:])
+
+        def pe_interleave(u):
+            banks = []
+            for y in range(3):
+                for pair in range(2):
+                    il = psum.tile([P, 2, DH, 4], BF16, name="il", tag="bank")
+                    for h in range(2):
+                        c0 = ((2 * pair + h) * 3 + y) * DH
+                        nc.tensor.matmul(
+                            il[:, h].rearrange("p i t -> p t i"),
+                            lhsT=ident16[:],
+                            rhs=wide[u][:, :, c0 : c0 + DH],
+                            start=True,
+                            stop=True,
+                        )
+                    banks.append(il)
+            return banks
+
+        def pe_copy(banks, y):
+            grouped = work.tile([P, BANK * 4], BF16, name="grouped", tag="slab", align_bytes=64)
+            for pair in range(2):
+                nc.scalar.copy(
+                    out=grouped[:, 1024 * pair : 1024 * (pair + 1)],
+                    in_=banks[2 * y + pair][:].rearrange("p h i t -> p (h i t)"),
+                )
+            return grouped
 
         def w_unit(u, fills):
             gq = interleave(u, 0)
@@ -204,31 +236,47 @@ def tile_mixerdiffattention_pa_kernel(tc, hidden_states, W_qkv_bytes, W_qkv_scal
         def nothing():
             return None
 
-        for a in range(NT):
-            x_transpose(a)
         widen(0, 0)
         tables_on_scalar()
-        for u in range(1, 4):
-            for t in range(4):
-                if (u, t) not in WIDEN_ON_VECTOR:
-                    widen(u, t)
-        for a in range(NT):
-            x_copy(a)
-        main_table()
         for t in range(1, 4):
             widen(0, t)
-
-        def wid(u, t):
-            return lambda: widen(u, t)
-
-        def xq(pair):
-            return lambda: x_quant(pair)
-
-        w_unit(0, ([wid(1, 2)], [wid(1, 3)], [], []))
-        w_unit(1, ([wid(2, 3)], [], [], []))
-        w_unit(2, ([], [], [], []))
-        w_unit(3, ([], [xq(0)], [xq(1)], [xq(2)]))
+        for t in range(4):
+            widen(1, t)
+        for t in range(4):
+            widen(2, t)
+        banks0 = pe_interleave(0)
+        g0 = [pe_copy(banks0, y) for y in range(3)]
+        for t in range(1, 4):
+            widen(3, t)
+        for y in range(3):
+            w_quant(0, y, g0[y])
+        for a in range(4):
+            x_transpose(a)
+        for a in range(4):
+            x_copy(a)
+        banks1 = pe_interleave(1)
+        widen(3, 0)
+        main_table()
+        x_quant(0)
+        i3 = [interleave(3, y) for y in range(3)]
+        g1 = [pe_copy(banks1, y) for y in range(3)]
+        for a in range(4, NT):
+            x_transpose(a)
+        for a in range(4, NT):
+            x_copy(a)
+        banks2 = pe_interleave(2)
+        for y in range(3):
+            w_quant(1, y, g1[y])
+        x_quant(1)
+        w_quant(3, 0, i3[0])
+        w_quant(3, 1, i3[1])
+        x_quant(2)
+        g2 = [pe_copy(banks2, y) for y in range(3)]
+        w_quant(2, 0, g2[0])
+        w_quant(3, 2, i3[2])
+        w_quant(2, 1, g2[1])
         x_quant(3)
+        w_quant(2, 2, g2[2])
 
         NJ = 8
         junk = keep.tile([P, NJ, DH], BF16, name="junk")
@@ -282,7 +330,7 @@ def tile_mixerdiffattention_pa_kernel(tc, hidden_states, W_qkv_bytes, W_qkv_scal
                     scale=1.0 / DH,
                     bias=EPS,
                 )
-                pq = work.tile([P, 8, 4 * HALF], F32, name="pq", tag="slab", align_bytes=64)
+                pq = big.tile([P, 8, 4 * HALF], F32, name="pq", tag="big")
                 for y in range(2):
                     for i in range(4):
                         nc.vector.scalar_tensor_tensor(

@@ -32,7 +32,7 @@ TWO_PI = 2.0 * math.pi
 MAGIC = 12582912.0
 
 UNITS = ((0, 0), (0, 1), (1, 0), (1, 1))
-WIDEN_ON_SCALAR = ((0, 0), (1, 0), (3, 0))
+WIDEN_ON_SCALAR = ((0, 0), (1, 0), (2, 0), (3, 0))
 TAIL_GROUPS_ON_VECTOR = 1
 
 
@@ -242,41 +242,42 @@ def tile_mixerdiffattention_pa_kernel(tc, hidden_states, W_qkv_bytes, W_qkv_scal
             widen(0, t)
         for t in range(4):
             widen(1, t)
-        for t in range(4):
-            widen(2, t)
-        banks0 = pe_interleave(0)
-        g0 = [pe_copy(banks0, y) for y in range(3)]
-        for t in range(1, 4):
-            widen(3, t)
-        for y in range(3):
-            w_quant(0, y, g0[y])
         for a in range(4):
             x_transpose(a)
+        widen(2, 0)
+        i0 = [interleave(0, 0), interleave(0, 1)]
         for a in range(4):
             x_copy(a)
         banks1 = pe_interleave(1)
-        widen(3, 0)
-        main_table()
+        w_quant(0, 0, i0[0])
+        i0.append(interleave(0, 2))
+        w_quant(0, 1, i0[1])
+        for t in range(1, 4):
+            widen(2, t)
+        w_quant(0, 2, i0[2])
         x_quant(0)
-        i3 = [interleave(3, y) for y in range(3)]
         g1 = [pe_copy(banks1, y) for y in range(3)]
-        for a in range(4, NT):
-            x_transpose(a)
-        for a in range(4, NT):
-            x_copy(a)
+        for t in range(4):
+            widen(3, t)
         banks2 = pe_interleave(2)
         for y in range(3):
             w_quant(1, y, g1[y])
         x_quant(1)
+        i3 = [interleave(3, y) for y in range(2)]
+        g2 = [pe_copy(banks2, y) for y in range(3)]
+        main_table()
+        for a in range(4, NT):
+            x_transpose(a)
+        for a in range(4, 6):
+            x_copy(a)
         w_quant(3, 0, i3[0])
+        w_quant(2, 0, g2[0])
+        i3.append(interleave(3, 2))
+        w_quant(2, 1, g2[1])
+        w_quant(2, 2, g2[2])
         w_quant(3, 1, i3[1])
         x_quant(2)
-        g2 = [pe_copy(banks2, y) for y in range(3)]
-        w_quant(2, 0, g2[0])
         w_quant(3, 2, i3[2])
-        w_quant(2, 1, g2[1])
-        x_quant(3)
-        w_quant(2, 2, g2[2])
 
         NJ = 8
         junk = keep.tile([P, NJ, DH], BF16, name="junk")
@@ -330,6 +331,9 @@ def tile_mixerdiffattention_pa_kernel(tc, hidden_states, W_qkv_bytes, W_qkv_scal
                     scale=1.0 / DH,
                     bias=EPS,
                 )
+                if group == 0:
+                    x_copy(6)
+                    x_copy(7)
                 pq = big.tile([P, 8, 4 * HALF], F32, name="pq", tag="big")
                 for y in range(2):
                     for i in range(4):
@@ -341,6 +345,8 @@ def tile_mixerdiffattention_pa_kernel(tc, hidden_states, W_qkv_bytes, W_qkv_scal
                             op0=ALU.mult,
                             op1=ALU.mult,
                         )
+                if group == 0:
+                    x_quant(3)
                 pairs = pq[:].rearrange("p i (h b j) -> p (i h) b j", h=2, b=2)
                 o = store.tile([P, 2, BANK], F32, name="o")
                 if group < 2 * NT - TAIL_GROUPS_ON_VECTOR:

@@ -34,6 +34,8 @@ MAGIC = 12582912.0
 UNITS = ((0, 0), (0, 1), (1, 0), (1, 1))
 WIDEN_ON_SCALAR = ((0, 0), (1, 0), (2, 0), (3, 0))
 TAIL_GROUPS_ON_VECTOR = 1
+FINE_GROUPS = 2
+LAST_PIECES = ((0, 0, 4), (1, 0, 2), (1, 2, 2))
 
 
 def tile_mixerdiffattention_pa_kernel(tc, hidden_states, W_qkv_bytes, W_qkv_scale, out_0, out_1, out_2):
@@ -91,16 +93,23 @@ def tile_mixerdiffattention_pa_kernel(tc, hidden_states, W_qkv_bytes, W_qkv_scal
         ident = keep.tile([P, P], F32, name="ident")
         make_identity(nc, ident[:])
         ident16 = keep.tile([P, P], BF16, name="ident16")
-        nc.gpsimd.tensor_scalar(out=ident16[:], in0=ident[:], scalar1=1.0, scalar2=0.0, op0=ALU.mult, op1=ALU.add)
+        nc.scalar.copy(out=ident16[:], in_=ident[:])
         one = keep.tile([P, 1], F32, name="one")
         nc.vector.memset(one[:], 1.0)
         freq = keep.tile([P, HALF], F32, name="freq")
-        nc.vector.tensor_scalar(out=freq[:, 0:1], in0=one[:], scalar1=1.0 / TWO_PI, scalar2=None, op0=ALU.mult)
-        for b in range(6):
-            n = 2**b
+        for j in range(4):
             nc.vector.tensor_scalar(
-                out=freq[:, n : 2 * n], in0=freq[:, 0:n], scalar1=10000.0 ** (-n / 64.0), scalar2=None, op0=ALU.mult
+                out=freq[:, j : j + 1], in0=one[:], scalar1=10000.0 ** (-j / 64.0) / TWO_PI, scalar2=None, op0=ALU.mult
             )
+        for n in (4, 16):
+            for i in range(1, 4):
+                nc.vector.tensor_scalar(
+                    out=freq[:, i * n : (i + 1) * n],
+                    in0=freq[:, 0:n],
+                    scalar1=10000.0 ** (-i * n / 64.0),
+                    scalar2=None,
+                    op0=ALU.mult,
+                )
         NA = NT * HALF
         turns = keep.tile([P, NT, HALF], F32, name="turns")
         nc.vector.tensor_tensor(
@@ -111,24 +120,25 @@ def tile_mixerdiffattention_pa_kernel(tc, hidden_states, W_qkv_bytes, W_qkv_scal
         )
         turns_f = turns[:].rearrange("p a j -> p (a j)")
         whole = keep.tile([P, NA], I32, name="whole")
-        nc.vector.tensor_scalar(out=whole[:], in0=turns_f, scalar1=-0.125, scalar2=MAGIC, op0=ALU.add, op1=ALU.add)
+        nc.vector.tensor_scalar(out=whole[:], in0=turns_f, scalar1=MAGIC, scalar2=None, op0=ALU.add)
         back = keep.tile([P, NA], F32, name="back")
         nc.vector.scalar_tensor_tensor(
             out=back[:], in0=whole[:], scalar=MAGIC, in1=turns_f, op0=ALU.subtract, op1=ALU.subtract
         )
-        mag = keep.tile([P, 2, NT, HALF], F32, name="mag")
+        mag = keep.tile([P, NA], F32, name="mag")
         cs = keep.tile([P, NT, 4, HALF], F32, name="cs")
 
         def tables_on_scalar():
-            nc.scalar.activation(out=mag[:, 0].rearrange("p a j -> p (a j)"), in_=back[:], func=ACT.Abs)
-            nc.scalar.activation(out=mag[:, 1].rearrange("p a j -> p (a j)"), in_=back[:], func=ACT.Abs, bias=0.25)
-            nc.scalar.activation(out=cs[:, :, 0, :], in_=mag[:, 0], func=ACT.Sin, scale=-TWO_PI, bias=0.5 * math.pi)
-            nc.scalar.activation(out=cs[:, :, 3, :], in_=mag[:, 0], func=ACT.Sin, scale=-TWO_PI, bias=0.5 * math.pi)
-            nc.scalar.activation(out=cs[:, :, 1, :], in_=mag[:, 1], func=ACT.Sin, scale=-TWO_PI, bias=0.5 * math.pi)
-            nc.scalar.activation(out=cs[:, :, 2, :], in_=mag[:, 1], func=ACT.Sin, scale=TWO_PI, bias=-0.5 * math.pi)
+            back3 = back[:].rearrange("p (a j) -> p a j", a=NT)
+            mag3 = mag[:].rearrange("p (a j) -> p a j", a=NT)
+            nc.scalar.activation(out=cs[:, :, 1, :], in_=back3, func=ACT.Sin, scale=-TWO_PI)
+            nc.scalar.activation(out=cs[:, :, 2, :], in_=back3, func=ACT.Sin, scale=TWO_PI)
+            nc.scalar.activation(out=mag[:], in_=back[:], func=ACT.Abs)
+            nc.scalar.activation(out=cs[:, :, 0, :], in_=mag3, func=ACT.Sin, scale=-TWO_PI, bias=0.5 * math.pi)
+            nc.scalar.activation(out=cs[:, :, 3, :], in_=mag3, func=ACT.Sin, scale=-TWO_PI, bias=0.5 * math.pi)
 
         def main_table():
-            nc.scalar.activation(out=warm[:], in_=mag[:, 1, 0, 0:1], func=ACT.Abs_reciprocal_sqrt, scale=1.0, bias=1.0)
+            nc.scalar.activation(out=warm[:], in_=cs[:, 0, 3, 0:1], func=ACT.Abs_reciprocal_sqrt, scale=1.0, bias=1.0)
 
         xc = keep.tile([P, NT, NG * P], U32, name="xc", align_bytes=64)
         xs = keep.tile([P, NT, NG * P], U8, name="xs", align_bytes=64)
@@ -208,14 +218,14 @@ def tile_mixerdiffattention_pa_kernel(tc, hidden_states, W_qkv_bytes, W_qkv_scal
                     banks.append(il)
             return banks
 
-        def pe_copy(banks, y):
-            grouped = work.tile([P, BANK * 4], BF16, name="grouped", tag="slab", align_bytes=64)
-            for pair in range(2):
-                nc.scalar.copy(
-                    out=grouped[:, 1024 * pair : 1024 * (pair + 1)],
-                    in_=banks[2 * y + pair][:].rearrange("p h i t -> p (h i t)"),
-                )
-            return grouped
+        def pe_copy(banks, slabs, b):
+            if b % 2 == 0:
+                grouped = work.tile([P, BANK * 4], BF16, name="grouped", tag="slab", align_bytes=64)
+                slabs.append(grouped)
+            nc.scalar.copy(
+                out=slabs[b // 2][:, 1024 * (b % 2) : 1024 * (b % 2 + 1)],
+                in_=banks[b][:].rearrange("p h i t -> p (h i t)"),
+            )
 
         def w_unit(u, fills):
             gq = interleave(u, 0)
@@ -238,10 +248,10 @@ def tile_mixerdiffattention_pa_kernel(tc, hidden_states, W_qkv_bytes, W_qkv_scal
 
         widen(0, 0)
         tables_on_scalar()
-        for t in range(1, 4):
-            widen(0, t)
-        for t in range(4):
-            widen(1, t)
+        for u in range(2):
+            for t in range(4):
+                if (u, t) != (0, 0):
+                    widen(u, t)
         for a in range(4):
             x_transpose(a)
         widen(2, 0)
@@ -256,15 +266,22 @@ def tile_mixerdiffattention_pa_kernel(tc, hidden_states, W_qkv_bytes, W_qkv_scal
             widen(2, t)
         w_quant(0, 2, i0[2])
         x_quant(0)
-        g1 = [pe_copy(banks1, y) for y in range(3)]
-        for t in range(4):
+        g1 = []
+        for b in range(3):
+            pe_copy(banks1, g1, b)
+        widen(3, 0)
+        for b in range(3, 6):
+            pe_copy(banks1, g1, b)
+        for t in range(1, 4):
             widen(3, t)
         banks2 = pe_interleave(2)
         for y in range(3):
             w_quant(1, y, g1[y])
         x_quant(1)
         i3 = [interleave(3, y) for y in range(2)]
-        g2 = [pe_copy(banks2, y) for y in range(3)]
+        g2 = []
+        for b in range(6):
+            pe_copy(banks2, g2, b)
         main_table()
         for a in range(4, NT):
             x_transpose(a)
@@ -349,22 +366,17 @@ def tile_mixerdiffattention_pa_kernel(tc, hidden_states, W_qkv_bytes, W_qkv_scal
                     x_quant(3)
                 pairs = pq[:].rearrange("p i (h b j) -> p (i h) b j", h=2, b=2)
                 o = store.tile([P, 2, BANK], F32, name="o")
+                flat = o[:].rearrange("p y (m j) -> p (y m) j", j=HALF)
                 if group < 2 * NT - TAIL_GROUPS_ON_VECTOR:
-                    nc.gpsimd.tensor_tensor(
-                        out=o[:].rearrange("p y (m j) -> p (y m) j", j=HALF),
-                        in0=pairs[:, :, 0, :],
-                        in1=pairs[:, :, 1, :],
-                        op=ALU.add,
-                    )
+                    banks = (slice(0, 16),) if group < 2 * NT - FINE_GROUPS else (slice(0, 8), slice(8, 16))
+                    for m in banks:
+                        nc.gpsimd.tensor_tensor(out=flat[:, m], in0=pairs[:, m, 0, :], in1=pairs[:, m, 1, :], op=ALU.add)
                     for y in range(2):
                         nc.sync.dma_start(out=outs[y][rows, cols], in_=o[:, y, :])
                 else:
-                    for y in range(2):
-                        nc.vector.tensor_tensor(
-                            out=o[:, y, :].rearrange("p (m j) -> p m j", j=HALF),
-                            in0=pairs[:, 8 * y : 8 * y + 8, 0, :],
-                            in1=pairs[:, 8 * y : 8 * y + 8, 1, :],
-                            op=ALU.add,
-                        )
-                        nc.sync.dma_start(out=outs[y][rows, cols], in_=o[:, y, :])
+                    for y, h, n in LAST_PIECES:
+                        m = slice(8 * y + 2 * h, 8 * y + 2 * (h + n))
+                        nc.vector.tensor_tensor(out=flat[:, m], in0=pairs[:, m, 0, :], in1=pairs[:, m, 1, :], op=ALU.add)
+                        c0 = half * BANK + DH * h
+                        nc.sync.dma_start(out=outs[y][rows, c0 : c0 + DH * n], in_=o[:, y, DH * h : DH * (h + n)])
                 group += 1

@@ -32,10 +32,8 @@ TWO_PI = 2.0 * math.pi
 MAGIC = 12582912.0
 
 UNITS = ((0, 0), (0, 1), (1, 0), (1, 1))
-WIDEN_ON_SCALAR = ((0, 0), (1, 0), (2, 0), (3, 0))
-TAIL_GROUPS_ON_VECTOR = 1
-FINE_GROUPS = 2
-LAST_PIECES = ((0, 0, 4), (1, 0, 2), (1, 2, 2))
+WIDEN_ON_SCALAR = ((0, 0), (1, 0), (3, 0))
+TAIL_GROUPS_ON_VECTOR = 2
 
 
 def tile_mixerdiffattention_pa_kernel(tc, hidden_states, W_qkv_bytes, W_qkv_scale, out_0, out_1, out_2):
@@ -274,6 +272,10 @@ def tile_mixerdiffattention_pa_kernel(tc, hidden_states, W_qkv_bytes, W_qkv_scal
             pe_copy(banks1, g1, b)
         for t in range(1, 4):
             widen(3, t)
+        for a in range(4, 6):
+            x_transpose(a)
+        for a in range(4, 6):
+            x_copy(a)
         banks2 = pe_interleave(2)
         for y in range(3):
             w_quant(1, y, g1[y])
@@ -283,9 +285,9 @@ def tile_mixerdiffattention_pa_kernel(tc, hidden_states, W_qkv_bytes, W_qkv_scal
         for b in range(6):
             pe_copy(banks2, g2, b)
         main_table()
-        for a in range(4, NT):
+        for a in range(6, NT):
             x_transpose(a)
-        for a in range(4, 6):
+        for a in range(6, NT):
             x_copy(a)
         w_quant(3, 0, i3[0])
         w_quant(2, 0, g2[0])
@@ -295,6 +297,7 @@ def tile_mixerdiffattention_pa_kernel(tc, hidden_states, W_qkv_bytes, W_qkv_scal
         w_quant(3, 1, i3[1])
         x_quant(2)
         w_quant(3, 2, i3[2])
+        x_quant(3)
 
         NJ = 8
         junk = keep.tile([P, NJ, DH], BF16, name="junk")
@@ -348,9 +351,6 @@ def tile_mixerdiffattention_pa_kernel(tc, hidden_states, W_qkv_bytes, W_qkv_scal
                     scale=1.0 / DH,
                     bias=EPS,
                 )
-                if group == 0:
-                    x_copy(6)
-                    x_copy(7)
                 pq = big.tile([P, 8, 4 * HALF], F32, name="pq", tag="big")
                 for y in range(2):
                     for i in range(4):
@@ -362,21 +362,21 @@ def tile_mixerdiffattention_pa_kernel(tc, hidden_states, W_qkv_bytes, W_qkv_scal
                             op0=ALU.mult,
                             op1=ALU.mult,
                         )
-                if group == 0:
-                    x_quant(3)
                 pairs = pq[:].rearrange("p i (h b j) -> p (i h) b j", h=2, b=2)
                 o = store.tile([P, 2, BANK], F32, name="o")
-                flat = o[:].rearrange("p y (m j) -> p (y m) j", j=HALF)
                 if group < 2 * NT - TAIL_GROUPS_ON_VECTOR:
-                    banks = (slice(0, 16),) if group < 2 * NT - FINE_GROUPS else (slice(0, 8), slice(8, 16))
-                    for m in banks:
+                    flat = o[:].rearrange("p y (m j) -> p (y m) j", j=HALF)
+                    for m in (slice(0, 8), slice(8, 16)) if group == 0 else (slice(0, 16),):
                         nc.gpsimd.tensor_tensor(out=flat[:, m], in0=pairs[:, m, 0, :], in1=pairs[:, m, 1, :], op=ALU.add)
                     for y in range(2):
                         nc.sync.dma_start(out=outs[y][rows, cols], in_=o[:, y, :])
                 else:
-                    for y, h, n in LAST_PIECES:
-                        m = slice(8 * y + 2 * h, 8 * y + 2 * (h + n))
-                        nc.vector.tensor_tensor(out=flat[:, m], in0=pairs[:, m, 0, :], in1=pairs[:, m, 1, :], op=ALU.add)
-                        c0 = half * BANK + DH * h
-                        nc.sync.dma_start(out=outs[y][rows, c0 : c0 + DH * n], in_=o[:, y, DH * h : DH * (h + n)])
+                    for y in range(2):
+                        nc.vector.tensor_tensor(
+                            out=o[:, y, :].rearrange("p (m j) -> p m j", j=HALF),
+                            in0=pairs[:, 8 * y : 8 * y + 8, 0, :],
+                            in1=pairs[:, 8 * y : 8 * y + 8, 1, :],
+                            op=ALU.add,
+                        )
+                        nc.sync.dma_start(out=outs[y][rows, cols], in_=o[:, y, :])
                 group += 1

@@ -32,8 +32,8 @@ TWO_PI = 2.0 * math.pi
 MAGIC = 12582912.0
 
 UNITS = ((0, 0), (0, 1), (1, 0), (1, 1))
-WIDEN_ON_SCALAR = ((0, 0), (1, 0), (3, 0))
-TAIL_GROUPS_ON_VECTOR = 2
+WIDEN_ON_SCALAR = ((0, 0), (1, 0), (2, 0), (3, 0))
+LATE_BANKS = 5
 
 
 def tile_mixerdiffattention_pa_kernel(tc, hidden_states, W_qkv_bytes, W_qkv_scale, out_0, out_1, out_2):
@@ -272,32 +272,27 @@ def tile_mixerdiffattention_pa_kernel(tc, hidden_states, W_qkv_bytes, W_qkv_scal
             pe_copy(banks1, g1, b)
         for t in range(1, 4):
             widen(3, t)
-        for a in range(4, 6):
+        for a in range(4, NT):
             x_transpose(a)
-        for a in range(4, 6):
+        for a in range(4, NT):
             x_copy(a)
+        main_table()
         banks2 = pe_interleave(2)
         for y in range(3):
             w_quant(1, y, g1[y])
         x_quant(1)
-        i3 = [interleave(3, y) for y in range(2)]
+        i3 = [interleave(3, y) for y in range(3)]
         g2 = []
         for b in range(6):
             pe_copy(banks2, g2, b)
-        main_table()
-        for a in range(6, NT):
-            x_transpose(a)
-        for a in range(6, NT):
-            x_copy(a)
         w_quant(3, 0, i3[0])
+        x_quant(2)
+        w_quant(3, 1, i3[1])
         w_quant(2, 0, g2[0])
-        i3.append(interleave(3, 2))
+        x_quant(3)
+        w_quant(3, 2, i3[2])
         w_quant(2, 1, g2[1])
         w_quant(2, 2, g2[2])
-        w_quant(3, 1, i3[1])
-        x_quant(2)
-        w_quant(3, 2, i3[2])
-        x_quant(3)
 
         NJ = 8
         junk = keep.tile([P, NJ, DH], BF16, name="junk")
@@ -319,6 +314,7 @@ def tile_mixerdiffattention_pa_kernel(tc, hidden_states, W_qkv_bytes, W_qkv_scal
                 )
             return acc
 
+        late = []
         group = 0
         for half in range(2):
             for a in range(NT):
@@ -364,19 +360,21 @@ def tile_mixerdiffattention_pa_kernel(tc, hidden_states, W_qkv_bytes, W_qkv_scal
                         )
                 pairs = pq[:].rearrange("p i (h b j) -> p (i h) b j", h=2, b=2)
                 o = store.tile([P, 2, BANK], F32, name="o")
-                if group < 2 * NT - TAIL_GROUPS_ON_VECTOR:
-                    flat = o[:].rearrange("p y (m j) -> p (y m) j", j=HALF)
-                    for m in (slice(0, 8), slice(8, 16)) if group == 0 else (slice(0, 16),):
+                flat = o[:].rearrange("p y (m j) -> p (y m) j", j=HALF)
+                ends = (8, 16) if group == 0 else (16,)
+                first_late = min(16, max(0, 8 * (4 * NT - LATE_BANKS - 2 * group)))
+                m0 = 0
+                for m1 in ends:
+                    m = slice(m0, min(m1, first_late))
+                    if m.stop > m.start:
                         nc.gpsimd.tensor_tensor(out=flat[:, m], in0=pairs[:, m, 0, :], in1=pairs[:, m, 1, :], op=ALU.add)
-                    for y in range(2):
+                    m0 = m1
+                for y in range(2):
+                    if 8 * y < first_late:
                         nc.sync.dma_start(out=outs[y][rows, cols], in_=o[:, y, :])
-                else:
-                    for y in range(2):
-                        nc.vector.tensor_tensor(
-                            out=o[:, y, :].rearrange("p (m j) -> p m j", j=HALF),
-                            in0=pairs[:, 8 * y : 8 * y + 8, 0, :],
-                            in1=pairs[:, 8 * y : 8 * y + 8, 1, :],
-                            op=ALU.add,
-                        )
-                        nc.sync.dma_start(out=outs[y][rows, cols], in_=o[:, y, :])
+                    else:
+                        late.append((pairs[:, 8 * y : 8 * y + 8], flat[:, 8 * y : 8 * y + 8], outs[y][rows, cols], o[:, y, :]))
                 group += 1
+        for both, total, where, row in late:
+            nc.vector.tensor_tensor(out=total, in0=both[:, :, 0, :], in1=both[:, :, 1, :], op=ALU.add)
+            nc.sync.dma_start(out=where, in_=row)

@@ -33,7 +33,9 @@ MAGIC = 12582912.0
 
 UNITS = ((0, 0), (0, 1), (1, 0), (1, 1))
 WIDEN_ON_SCALAR = ((0, 0), (1, 0), (2, 0), (3, 0))
-LATE_BANKS = 5
+STORE_LAG = 2
+LATE_GROUPS = 3
+LATE_ADDERS = ("tensor", "tensor", "gpsimd", "gpsimd", "vector", "vector")
 
 
 def tile_mixerdiffattention_pa_kernel(tc, hidden_states, W_qkv_bytes, W_qkv_scale, out_0, out_1, out_2):
@@ -315,6 +317,7 @@ def tile_mixerdiffattention_pa_kernel(tc, hidden_states, W_qkv_bytes, W_qkv_scal
             return acc
 
         late = []
+        waiting = []
         group = 0
         for half in range(2):
             for a in range(NT):
@@ -339,6 +342,9 @@ def tile_mixerdiffattention_pa_kernel(tc, hidden_states, W_qkv_bytes, W_qkv_scal
                 ov = store.tile([P, BANK], F32, name="ov")
                 nc.scalar.copy(out=ov[:], in_=accv[:])
                 nc.sync.dma_start(out=outs[2][rows, cols], in_=ov[:])
+                if group >= STORE_LAG and waiting:
+                    for where, row in waiting.pop(0):
+                        nc.sync.dma_start(out=where, in_=row)
                 first = 2 * group + (1 if group == 0 else 0)
                 nc.scalar.activation(
                     out=rn_all[:, first : 2 * group + 2, :],
@@ -361,20 +367,26 @@ def tile_mixerdiffattention_pa_kernel(tc, hidden_states, W_qkv_bytes, W_qkv_scal
                 pairs = pq[:].rearrange("p i (h b j) -> p (i h) b j", h=2, b=2)
                 o = store.tile([P, 2, BANK], F32, name="o")
                 flat = o[:].rearrange("p y (m j) -> p (y m) j", j=HALF)
-                ends = (8, 16) if group == 0 else (16,)
-                first_late = min(16, max(0, 8 * (4 * NT - LATE_BANKS - 2 * group)))
-                m0 = 0
-                for m1 in ends:
-                    m = slice(m0, min(m1, first_late))
-                    if m.stop > m.start:
+                if group < 2 * NT - LATE_GROUPS:
+                    for m in (slice(0, 8), slice(8, 16)) if group == 0 else (slice(0, 16),):
                         nc.gpsimd.tensor_tensor(out=flat[:, m], in0=pairs[:, m, 0, :], in1=pairs[:, m, 1, :], op=ALU.add)
-                    m0 = m1
-                for y in range(2):
-                    if 8 * y < first_late:
-                        nc.sync.dma_start(out=outs[y][rows, cols], in_=o[:, y, :])
-                    else:
-                        late.append((pairs[:, 8 * y : 8 * y + 8], flat[:, 8 * y : 8 * y + 8], outs[y][rows, cols], o[:, y, :]))
+                    waiting.append([(outs[y][rows, cols], o[:, y, :]) for y in range(2)])
+                else:
+                    for y in range(2):
+                        m = slice(8 * y, 8 * y + 8)
+                        late.append((pairs[:, m], flat[:, m], o[:, y, :], outs[y][rows, cols]))
                 group += 1
-        for both, total, where, row in late:
-            nc.vector.tensor_tensor(out=total, in0=both[:, :, 0, :], in1=both[:, :, 1, :], op=ALU.add)
+        for stores in waiting:
+            for where, row in stores:
+                nc.sync.dma_start(out=where, in_=row)
+        for (both, total, row, where), adder in zip(late, LATE_ADDERS):
+            if adder == "tensor":
+                added = psum.tile([P, 8, HALF], F32, name="added", tag="bank")
+                for b in range(2):
+                    nc.tensor.matmul(added[:], lhsT=ident[:], rhs=both[:, :, b, :], start=(b == 0), stop=(b == 1))
+                nc.scalar.copy(out=total, in_=added[:])
+            elif adder == "gpsimd":
+                nc.gpsimd.tensor_tensor(out=total, in0=both[:, :, 0, :], in1=both[:, :, 1, :], op=ALU.add)
+            else:
+                nc.vector.tensor_tensor(out=total, in0=both[:, :, 0, :], in1=both[:, :, 1, :], op=ALU.add)
             nc.sync.dma_start(out=where, in_=row)

@@ -78,9 +78,9 @@ def tile_mixerdiffattention_pa_kernel(tc, hidden_states, W_qkv_bytes, W_qkv_scal
         for t in range(4):
             nc.sync.dma_start(out=wbytes[0][:, t, 0:HW], in_=w_dram[0][:, t, 0:HW])
         load_w(1)
-        load_w(2)
         load_x(0, 2)
         load_x(2, 2)
+        load_w(2)
         load_w(3)
         load_x(4, 2)
         load_x(6, 2)
@@ -254,10 +254,10 @@ def tile_mixerdiffattention_pa_kernel(tc, hidden_states, W_qkv_bytes, W_qkv_scal
                     widen(u, t)
         for a in range(4):
             x_transpose(a)
-        widen(2, 0)
         i0 = [interleave(0, 0), interleave(0, 1)]
         for a in range(4):
             x_copy(a)
+        widen(2, 0)
         banks1 = pe_interleave(1)
         w_quant(0, 0, i0[0])
         i0.append(interleave(0, 2))

@@ -191,8 +191,8 @@ def tile_mixerdiffattention_pa_kernel(tc, hidden_states, W_qkv_bytes, W_qkv_scal
         def interleave(u, y):
             grouped = work.tile([P, BANK * 4], BF16, name="grouped", tag="slab", align_bytes=64)
             nc.vector.tensor_copy(
-                out=grouped[:].rearrange("p (h c i t) -> p h c t i", h=4, c=DH // 4, i=4, t=4),
-                in_=wide[u][:].rearrange("p t (h y c i) -> p y h c t i", h=4, y=3, c=DH // 4, i=4)[:, y],
+                out=grouped[:].rearrange("p (h c i t) -> p h c t i", h=4, c=DH // 8, i=8, t=4),
+                in_=wide[u][:].rearrange("p t (h y c i) -> p y h c t i", h=4, y=3, c=DH // 8, i=8)[:, y],
             )
             return grouped
 

import math
from contextlib import ExitStack

import concourse.mybir as mybir
from concourse.masks import make_identity

F32 = mybir.dt.float32
BF16 = mybir.dt.bfloat16
I32 = mybir.dt.int32
U32 = mybir.dt.uint32
U8 = mybir.dt.uint8
FP8 = mybir.dt.float8_e4m3fn
FP8X4 = mybir.dt.float8_e4m3fn_x4
ALU = mybir.AluOpType
ACT = mybir.ActivationFunctionType

P = 128
T = 1024
D = 1024
DH = 128
HALF = 64
NT = T // P
NG = D // 512
NCOL = 3 * D
HW = NCOL // 2
BANK = 512
EPS = 1e-6

FLOPS = 2 * T * D * NCOL

TWO_PI = 2.0 * math.pi
MAGIC = 12582912.0

UNITS = ((0, 0), (0, 1), (1, 0), (1, 1))
WIDEN_ON_SCALAR = ((0, 0), (1, 0), (2, 0), (3, 0))
STORE_LAG = 2
LATE_GROUPS = 3
LATE_ADDERS = ("tensor", "tensor", "gpsimd", "gpsimd", "vector", "vector")


def tile_mixerdiffattention_pa_kernel(tc, hidden_states, W_qkv_bytes, W_qkv_scale, out_0, out_1, out_2):
    nc = tc.nc
    x_dram = hidden_states.rearrange("b t k -> (b t) k")
    w_dram = W_qkv_bytes.rearrange("(g p t) n -> g p t n", g=NG, p=P, t=4)
    s_dram = W_qkv_scale.rearrange("(g p t) o -> p g (t o)", g=NG, p=P, t=4)
    outs = [
        out_0.rearrange("b t h d -> (b t) (h d)"),
        out_1.rearrange("b t h d -> (b t) (h d)"),
        out_2.rearrange("b t h d -> (b t) (h d)"),
    ]

    with ExitStack() as ctx:
        keep = ctx.enter_context(tc.tile_pool(name="keep", bufs=1))
        big = ctx.enter_context(tc.tile_pool(name="big", bufs=4))
        work = ctx.enter_context(tc.tile_pool(name="work", bufs=6))
        xwork = ctx.enter_context(tc.tile_pool(name="xwork", bufs=4))
        store = ctx.enter_context(tc.tile_pool(name="store", bufs=4))
        psum = ctx.enter_context(tc.psum_pool(name="psum", bufs=8))
        ctx.enter_context(tc.manual_schedule())

        wsc = keep.tile([P, NG, 4], F32, name="wsc")
        nc.sync.dma_start(out=wsc[:], in_=s_dram)
        wbytes = [keep.tile([P, 4, NCOL], U8, name="wbytes%d" % g) for g in range(NG)]
        x_all = keep.tile([P, NT, D], BF16, name="x_all")

        def load_w(u):
            half, g = UNITS[u]
            nc.sync.dma_start(
                out=wbytes[g][:, :, half * HW : (half + 1) * HW], in_=w_dram[g][:, :, half * HW : (half + 1) * HW]
            )

        def load_x(a0, n):
            nc.sync.dma_start(
                out=x_all[:, a0 : a0 + n, :],
                in_=x_dram[a0 * P : (a0 + n) * P, :].rearrange("(a p) k -> p a k", p=P),
            )

        for t in range(4):
            nc.sync.dma_start(out=wbytes[0][:, t, 0:HW], in_=w_dram[0][:, t, 0:HW])
        load_w(1)
        load_x(0, 2)
        load_x(2, 2)
        load_w(2)
        load_w(3)
        load_x(4, 2)
        load_x(6, 2)

        warm = keep.tile([P, 1], F32, name="warm")
        nc.vector.memset(warm[:], 0.0)
        nc.scalar.activation(out=warm[:], in_=warm[:], func=ACT.Sin)
        tpos = keep.tile([P, NT], F32, name="tpos")
        nc.gpsimd.iota(tpos[:], pattern=[[P, NT]], base=0, channel_multiplier=1, allow_small_or_imprecise_dtypes=True)
        ident = keep.tile([P, P], F32, name="ident")
        make_identity(nc, ident[:])
        ident16 = keep.tile([P, P], BF16, name="ident16")
        nc.scalar.copy(out=ident16[:], in_=ident[:])
        one = keep.tile([P, 1], F32, name="one")
        nc.vector.memset(one[:], 1.0)
        freq = keep.tile([P, HALF], F32, name="freq")
        for j in range(4):
            nc.vector.tensor_scalar(
                out=freq[:, j : j + 1], in0=one[:], scalar1=10000.0 ** (-j / 64.0) / TWO_PI, scalar2=None, op0=ALU.mult
            )
        for n in (4, 16):
            for i in range(1, 4):
                nc.vector.tensor_scalar(
                    out=freq[:, i * n : (i + 1) * n],
                    in0=freq[:, 0:n],
                    scalar1=10000.0 ** (-i * n / 64.0),
                    scalar2=None,
                    op0=ALU.mult,
                )
        NA = NT * HALF
        turns = keep.tile([P, NT, HALF], F32, name="turns")
        nc.vector.tensor_tensor(
            out=turns[:],
            in0=freq[:].unsqueeze(1).to_broadcast([P, NT, HALF]),
            in1=tpos[:].unsqueeze(2).to_broadcast([P, NT, HALF]),
            op=ALU.mult,
        )
        turns_f = turns[:].rearrange("p a j -> p (a j)")
        whole = keep.tile([P, NA], I32, name="whole")
        nc.vector.tensor_scalar(out=whole[:], in0=turns_f, scalar1=MAGIC, scalar2=None, op0=ALU.add)
        back = keep.tile([P, NA], F32, name="back")
        nc.vector.scalar_tensor_tensor(
            out=back[:], in0=whole[:], scalar=MAGIC, in1=turns_f, op0=ALU.subtract, op1=ALU.subtract
        )
        mag = keep.tile([P, NA], F32, name="mag")
        cs = keep.tile([P, NT, 4, HALF], F32, name="cs")

        def tables_on_scalar():
            back3 = back[:].rearrange("p (a j) -> p a j", a=NT)
            mag3 = mag[:].rearrange("p (a j) -> p a j", a=NT)
            nc.scalar.activation(out=cs[:, :, 1, :], in_=back3, func=ACT.Sin, scale=-TWO_PI)
            nc.scalar.activation(out=cs[:, :, 2, :], in_=back3, func=ACT.Sin, scale=TWO_PI)
            nc.scalar.activation(out=mag[:], in_=back[:], func=ACT.Abs)
            nc.scalar.activation(out=cs[:, :, 0, :], in_=mag3, func=ACT.Sin, scale=-TWO_PI, bias=0.5 * math.pi)
            nc.scalar.activation(out=cs[:, :, 3, :], in_=mag3, func=ACT.Sin, scale=-TWO_PI, bias=0.5 * math.pi)

        def main_table():
            nc.scalar.activation(out=warm[:], in_=cs[:, 0, 3, 0:1], func=ACT.Abs_reciprocal_sqrt, scale=1.0, bias=1.0)

        xc = keep.tile([P, NT, NG * P], U32, name="xc", align_bytes=64)
        xs = keep.tile([P, NT, NG * P], U8, name="xs", align_bytes=64)
        xts = []
        xgs = []

        def x_transpose(a):
            words = x_all[:, a, :].bitcast(F32)
            xt = psum.tile([P, NG, 2, P], F32, name="xt", tag="bank")
            for g in range(NG):
                for u in range(2):
                    nc.tensor.transpose(xt[:, g, u, :], words[:, 256 * g + u : 256 * (g + 1) : 2], ident[:])
            xts.append(xt)

        def x_copy(a):
            if a % 2 == 0:
                xg_new = xwork.tile([P, 2, NG * P * 4], BF16, name="xg", align_bytes=64)
                xgs.append(xg_new)
            xg = xgs[a // 2]
            dst = xg[:, a % 2, :].bitcast(F32).rearrange("p (g r u) -> p g r u", g=NG, u=2)
            src = xts[a][:].rearrange("p g u r -> p g r u")
            nc.scalar.copy(out=dst, in_=src)

        def x_quant(pair):
            nc.vector.quantize_mx(
                out=xc[:, 2 * pair : 2 * pair + 2, :].rearrange("p a c -> p (a c)").bitcast(FP8X4),
                scales=xs[:, 2 * pair : 2 * pair + 2, :].rearrange("p a c -> p (a c)"),
                in_=xgs[pair][:].rearrange("p a c -> p (a c)"),
            )

        wide = []
        for u in range(4):
            wide_u = big.tile([P, 4, HW], BF16, name="wide_u", tag="big")
            wide.append(wide_u)
        wcodes = keep.tile([P, NG * 6 * BANK], U32, name="wcodes", align_bytes=64)
        wscl = keep.tile([P, NG * 6 * BANK], U8, name="wscl", align_bytes=64)

        def chunk(g, y, half):
            c0 = ((g * 3 + y) * 2 + half) * BANK
            return slice(c0, c0 + BANK)

        def widen(u, t):
            half, g = UNITS[u]
            src = wbytes[g][:, t, half * HW : (half + 1) * HW].bitcast(FP8)
            if (u, t) not in WIDEN_ON_SCALAR:
                nc.vector.tensor_scalar(out=wide[u][:, t, :], in0=src, scalar1=wsc[:, g, t : t + 1], scalar2=None, op0=ALU.mult)
            else:
                nc.scalar.activation(out=wide[u][:, t, :], in_=src, func=ACT.Copy, scale=wsc[:, g, t : t + 1])

        def interleave(u, y):
            grouped = work.tile([P, BANK * 4], BF16, name="grouped", tag="slab", align_bytes=64)
            nc.vector.tensor_copy(
                out=grouped[:].rearrange("p (h c i t) -> p h c t i", h=4, c=DH // 8, i=8, t=4),
                in_=wide[u][:].rearrange("p t (h y c i) -> p y h c t i", h=4, y=3, c=DH // 8, i=8)[:, y],
            )
            return grouped

        def w_quant(u, y, grouped):
            half, g = UNITS[u]
            cols = chunk(g, y, half)
            nc.vector.quantize_mx(out=wcodes[:, cols].bitcast(FP8X4), scales=wscl[:, cols], in_=grouped[:])

        def pe_interleave(u):
            banks = []
            for y in range(3):
                for pair in range(2):
                    il = psum.tile([P, 2, DH, 4], BF16, name="il", tag="bank")
                    for h in range(2):
                        c0 = ((2 * pair + h) * 3 + y) * DH
                        nc.tensor.matmul(
                            il[:, h].rearrange("p i t -> p t i"),
                            lhsT=ident16[:],
                            rhs=wide[u][:, :, c0 : c0 + DH],
                            start=True,
                            stop=True,
                        )
                    banks.append(il)
            return banks

        def pe_copy(banks, slabs, b):
            if b % 2 == 0:
                grouped = work.tile([P, BANK * 4], BF16, name="grouped", tag="slab", align_bytes=64)
                slabs.append(grouped)
            nc.scalar.copy(
                out=slabs[b // 2][:, 1024 * (b % 2) : 1024 * (b % 2 + 1)],
                in_=banks[b][:].rearrange("p h i t -> p (h i t)"),
            )

        def w_unit(u, fills):
            gq = interleave(u, 0)
            for f in fills[0]:
                f()
            gk = interleave(u, 1)
            for f in fills[1]:
                f()
            w_quant(u, 0, gq)
            gv = interleave(u, 2)
            for f in fills[2]:
                f()
            w_quant(u, 1, gk)
            for f in fills[3]:
                f()
            w_quant(u, 2, gv)

        def nothing():
            return None

        widen(0, 0)
        tables_on_scalar()
        for u in range(2):
            for t in range(4):
                if (u, t) != (0, 0):
                    widen(u, t)
        for a in range(4):
            x_transpose(a)
        i0 = [interleave(0, 0), interleave(0, 1)]
        for a in range(4):
            x_copy(a)
        widen(2, 0)
        banks1 = pe_interleave(1)
        w_quant(0, 0, i0[0])
        i0.append(interleave(0, 2))
        w_quant(0, 1, i0[1])
        for t in range(1, 4):
            widen(2, t)
        w_quant(0, 2, i0[2])
        x_quant(0)
        g1 = []
        for b in range(3):
            pe_copy(banks1, g1, b)
        widen(3, 0)
        for b in range(3, 6):
            pe_copy(banks1, g1, b)
        for t in range(1, 4):
            widen(3, t)
        for a in range(4, NT):
            x_transpose(a)
        for a in range(4, NT):
            x_copy(a)
        main_table()
        banks2 = pe_interleave(2)
        for y in range(3):
            w_quant(1, y, g1[y])
        x_quant(1)
        i3 = [interleave(3, y) for y in range(3)]
        g2 = []
        for b in range(6):
            pe_copy(banks2, g2, b)
        w_quant(3, 0, i3[0])
        x_quant(2)
        w_quant(3, 1, i3[1])
        w_quant(2, 0, g2[0])
        x_quant(3)
        w_quant(3, 2, i3[2])
        w_quant(2, 1, g2[1])
        w_quant(2, 2, g2[2])

        NJ = 8
        junk = keep.tile([P, NJ, DH], BF16, name="junk")
        ss_all = keep.tile([P, 2 * NT * 2, 4], F32, name="ss_all")
        rn_all = keep.tile([P, 2 * NT * 2, 4], F32, name="rn_all")

        def mx(a, y, half):
            acc = psum.tile([P, BANK], F32, name="acc", tag="bank")
            for g in range(NG):
                cols = chunk(g, y, half)
                nc.tensor.matmul_mx(
                    out=acc[:],
                    lhsT=xc[:, a, g * P : (g + 1) * P].bitcast(FP8X4),
                    lhsT_scale=xs[:, a, g * P : (g + 1) * P],
                    rhs=wcodes[:, cols].bitcast(FP8X4),
                    rhs_scale=wscl[:, cols],
                    start=(g == 0),
                    stop=(g == NG - 1),
                )
            return acc

        late = []
        waiting = []
        group = 0
        for half in range(2):
            for a in range(NT):
                rows = slice(a * P, (a + 1) * P)
                cols = slice(half * BANK, (half + 1) * BANK)
                accv = mx(a, 2, half)
                accs = []
                for y in range(2):
                    acc = mx(a, y, half)
                    for i in range(4):
                        nc.scalar.activation(
                            out=junk[:, (4 * y + i) % NJ, :],
                            in_=acc[:, i * DH : (i + 1) * DH],
                            func=ACT.Square,
                            accum_out=ss_all[:, 2 * group + y, i : i + 1],
                        )
                    accs.append(acc)
                    if group == 0 and y == 0:
                        nc.scalar.activation(
                            out=rn_all[:, 0, :], in_=ss_all[:, 0, :], func=ACT.Abs_reciprocal_sqrt, scale=1.0 / DH, bias=EPS
                        )
                ov = store.tile([P, BANK], F32, name="ov")
                nc.scalar.copy(out=ov[:], in_=accv[:])
                nc.sync.dma_start(out=outs[2][rows, cols], in_=ov[:])
                if group >= STORE_LAG and waiting:
                    for where, row in waiting.pop(0):
                        nc.sync.dma_start(out=where, in_=row)
                first = 2 * group + (1 if group == 0 else 0)
                nc.scalar.activation(
                    out=rn_all[:, first : 2 * group + 2, :],
                    in_=ss_all[:, first : 2 * group + 2, :],
                    func=ACT.Abs_reciprocal_sqrt,
                    scale=1.0 / DH,
                    bias=EPS,
                )
                pq = big.tile([P, 8, 4 * HALF], F32, name="pq", tag="big")
                for y in range(2):
                    for i in range(4):
                        nc.vector.scalar_tensor_tensor(
                            out=pq[:, 4 * y + i, :].rearrange("p (r c) -> p r c", r=2),
                            in0=accs[y][:, i * DH : (i + 1) * DH].unsqueeze(1).to_broadcast([P, 2, DH]),
                            scalar=rn_all[:, 2 * group + y, i : i + 1],
                            in1=cs[:, a].rearrange("p (r b) j -> p r (b j)", r=2),
                            op0=ALU.mult,
                            op1=ALU.mult,
                        )
                pairs = pq[:].rearrange("p i (h b j) -> p (i h) b j", h=2, b=2)
                o = store.tile([P, 2, BANK], F32, name="o")
                flat = o[:].rearrange("p y (m j) -> p (y m) j", j=HALF)
                if group < 2 * NT - LATE_GROUPS:
                    for m in (slice(0, 8), slice(8, 16)) if group == 0 else (slice(0, 16),):
                        nc.gpsimd.tensor_tensor(out=flat[:, m], in0=pairs[:, m, 0, :], in1=pairs[:, m, 1, :], op=ALU.add)
                    waiting.append([(outs[y][rows, cols], o[:, y, :]) for y in range(2)])
                else:
                    for y in range(2):
                        m = slice(8 * y, 8 * y + 8)
                        late.append((pairs[:, m], flat[:, m], o[:, y, :], outs[y][rows, cols]))
                group += 1
        for stores in waiting:
            for where, row in stores:
                nc.sync.dma_start(out=where, in_=row)
        for (both, total, row, where), adder in zip(late, LATE_ADDERS):
            if adder == "tensor":
                added = psum.tile([P, 8, HALF], F32, name="added", tag="bank")
                for b in range(2):
                    nc.tensor.matmul(added[:], lhsT=ident[:], rhs=both[:, :, b, :], start=(b == 0), stop=(b == 1))
                nc.scalar.copy(out=total, in_=added[:])
            elif adder == "gpsimd":
                nc.gpsimd.tensor_tensor(out=total, in0=both[:, :, 0, :], in1=both[:, :, 1, :], op=ALU.add)
            else:
                nc.vector.tensor_tensor(out=total, in0=both[:, :, 0, :], in1=both[:, :, 1, :], op=ALU.add)
            nc.sync.dma_start(out=where, in_=row)
